import numpy as np
import ml_dtypes


def mxq(x, axis, fmt="e4m3"):
    dtype, down = {"e4m3": (ml_dtypes.float8_e4m3fn, 7), "e5m2": (ml_dtypes.float8_e5m2, 14)}[fmt]
    v = np.moveaxis(np.asarray(x, np.float32).astype(ml_dtypes.bfloat16).astype(np.float64), axis, -1)
    blocks = v.reshape(v.shape[:-1] + (-1, 32))
    amax = np.abs(blocks).max(-1, keepdims=True)
    byte = np.maximum(np.where(amax > 0, np.frexp(amax)[1] - 1 + 127, 0) - down, 1)
    scale = np.exp2(byte - 127.0)
    codes = (blocks / scale).astype(np.float32).astype(dtype).astype(np.float64)
    return np.moveaxis((codes * scale).reshape(v.shape), -1, axis)


WIDE = False


def mx_kscale(k):
    if not WIDE:
        return np.ones(k)
    levels = np.array([10, -10, 5, -5, 0])
    a = np.random.permutation(np.resize(levels, k // 512 * 4)).reshape(k // 512, 4)
    idx = np.arange(k)
    return np.exp2(a[idx // 512, idx % 128 // 32])


BF16 = ml_dtypes.bfloat16


def bf(x):
    return np.asarray(x, np.float32).astype(BF16)


def f64(x):
    return np.asarray(x).astype(np.float64)


B, IN, NLVL, KLVL, C, CM, CO, OU, OV = 2, 256, 5, 3, 128, 128, 32, 8, 8
P = 2 ** (KLVL - 2)
S = 2 ** (NLVL - KLVL + 2)
KA, KB = 4 * C, 4 * CM


def patches(x):
    U, V, Bn, H, W, Cc = x.shape
    return x.reshape(U, V, Bn, H // 2, 2, W // 2, 2, Cc).swapaxes(4, 5).reshape(U, V, Bn * (H // 2) * (W // 2), 4 * Cc)


def branch_conv(x, w, b):
    U, V, Bn, H, W, Cc = x.shape
    Co = w.shape[-1]
    R = Bn * (H // 2) * (W // 2)
    p = patches(x).reshape(U, 1, V, 1, R, 4 * Cc)
    wc = w.reshape(U, 2, V, 2, 4 * Cc, Co)
    y = (mxq(p, 5, "e4m3") @ mxq(wc, 4, "e4m3")) + b.reshape(U, 2, V, 2, 1, Co)
    return np.maximum(y, 0.0).reshape(2 * U, 2 * V, Bn, H // 2, W // 2, Co)


def setup_inputs():
    s = mx_kscale(KA).reshape(2, 2, C)
    t = mx_kscale(KB)[:CM]
    x = np.maximum(np.random.standard_normal((P, P, B, S, S, C)), 0.0) * np.tile(s, (S // 2, S // 2, 1))
    return {"x_parent": bf(x),
            "f_child": bf(np.random.standard_normal((2 * P, 2 * P, 2, 2, C, CM)) * np.sqrt(0.5 / C) / s[:, :, :, None] * t),
            "b_child": bf(np.random.standard_normal((2 * P, 2 * P, CM)) * 0.2 * t),
            "f_gchild": bf(np.random.standard_normal((4 * P, 4 * P, 2, 2, CM, CO)) * np.sqrt(0.5 / CM) / t[:, None]),
            "b_gchild": bf(np.random.standard_normal((4 * P, 4 * P, CO)) * 0.2)}


def reference(x_parent, f_child, b_child, f_gchild, b_gchild):
    h = branch_conv(f64(x_parent), f64(f_child), f64(b_child))
    return branch_conv(h, f64(f_gchild), f64(b_gchild))

@@ -1,0 +1,217 @@
+from contextlib import ExitStack
+
+import concourse.mybir as mybir
+from concourse.masks import make_identity
+
+F32 = mybir.dt.float32
+BF16 = mybir.dt.bfloat16
+U32 = mybir.dt.uint32
+U8 = mybir.dt.uint8
+FP8X4 = mybir.dt.float8_e4m3fn_x4
+ADD = mybir.AluOpType.add
+RELU = mybir.ActivationFunctionType.Relu
+
+P = 128
+PACK = 4
+K = P * PACK
+GRID1 = 4
+C_MID = 128
+C_OUT = 32
+ROWS1 = 128
+ROWS2 = 32
+HI = C_MID // PACK
+
+FLOPS = 2 * 16 * ROWS1 * K * C_MID + 2 * 64 * ROWS2 * K * C_OUT
+
+
+def tile_butterflylayer2d_pa_s_kernel(tc, x_parent, f_child, b_child, f_gchild, b_gchild, out):
+    nc = tc.nc
+    with ExitStack() as ctx:
+        keep = ctx.enter_context(tc.tile_pool(name="keep", bufs=1))
+        work = ctx.enter_context(tc.tile_pool(name="work", bufs=2))
+        psum_prep = ctx.enter_context(tc.psum_pool(name="psum_prep", bufs=1))
+        psum_x = ctx.enter_context(tc.psum_pool(name="psum_x", bufs=2))
+        psum_h = ctx.enter_context(tc.psum_pool(name="psum_h", bufs=2))
+        psum_o = ctx.enter_context(tc.psum_pool(name="psum_o", bufs=2))
+
+        x_rows = keep.tile([P, 4, K], BF16)
+        patches = x_parent.rearrange("u v n (y p) (s d q) c -> d p (u v n y) s (q c)", p=2, s=4, d=2)
+        for d in range(2):
+            for p in range(2):
+                nc.sync.dma_start(out=x_rows[d:P:2, :, p * 256 : (p + 1) * 256], in_=patches[d, p])
+
+        fc_raw = keep.tile([P, GRID1, GRID1, PACK * C_MID], BF16)
+        for i in range(GRID1):
+            nc.sync.dma_start(
+                out=fc_raw[:, i], in_=f_child[i].rearrange("j p q (h l) o -> (p q h) j (l o)", l=PACK)
+            )
+        gc_raw = keep.tile([P, GRID1, 16, PACK * C_OUT], BF16)
+        for i in range(GRID1):
+            nc.sync.dma_start(
+                out=gc_raw[:, i],
+                in_=f_gchild[2 * i : 2 * i + 2].rearrange("a j p q (h l) o -> (p q h) (a j) (l o)", l=PACK),
+            )
+
+        bc_rows = keep.tile([P, 16 * PACK], BF16)
+        nc.vector.memset(bc_rows[:], 0.0)
+        nc.scalar.dma_start(
+            out=bc_rows[0:HI, :].rearrange("h (n l) -> h n l", l=PACK),
+            in_=b_child.rearrange("i j (h l) -> h (i j) l", l=PACK),
+        )
+        bg_rows = keep.tile([P, 8 * 2 * C_OUT], BF16)
+        nc.vector.memset(bg_rows[:], 0.0)
+        nc.scalar.dma_start(
+            out=bg_rows[0:GRID1, :].rearrange("j (i f) -> j i f", i=8),
+            in_=b_gchild.rearrange("i (j e) o -> j i (e o)", e=2),
+        )
+
+        ident = keep.tile([P, P], F32)
+        make_identity(nc, ident[:])
+        spread_c = keep.tile([P, P], BF16)
+        nc.vector.tensor_copy(
+            out=spread_c[:].rearrange("k (t h) -> k t h", t=4),
+            in_=ident[:, 0:HI].unsqueeze(1).to_broadcast([P, 4, HI]),
+        )
+        spread_g = keep.tile([P, P], BF16)
+        nc.vector.tensor_copy(
+            out=spread_g[:].rearrange("k (j w) -> k j w", j=GRID1),
+            in_=ident[:, 0:GRID1].unsqueeze(2).to_broadcast([P, GRID1, ROWS2]),
+        )
+        sort_pixels = keep.tile([P, P], F32)
+        nc.vector.tensor_copy(
+            out=sort_pixels[:].rearrange("r (g t a) -> r g t a", g=4, t=4),
+            in_=ident[:].rearrange("r (g a t) -> r g t a", g=4, t=4),
+        )
+
+        bc_ps = psum_prep.tile([P, 16 * PACK], F32)
+        nc.tensor.matmul(out=bc_ps[:], lhsT=spread_c[:], rhs=bc_rows[:], start=True, stop=True)
+        bias_c = keep.tile([P, 16 * PACK], F32)
+        nc.vector.tensor_copy(out=bias_c[:], in_=bc_ps[:])
+        bg_ps = psum_prep.tile([P, 8 * 2 * C_OUT], F32)
+        nc.tensor.matmul(out=bg_ps[:], lhsT=spread_g[:], rhs=bg_rows[:], start=True, stop=True)
+        bias_g = keep.tile([P, 8 * 2 * C_OUT], F32)
+        nc.scalar.copy(out=bias_g[:], in_=bg_ps[:])
+
+        x_words = x_rows[:].bitcast(F32).rearrange("c s (k v) -> c s k v", v=2)
+        x_grp = keep.tile([P, 4 * ROWS1 * PACK], BF16, align_bytes=64)
+        x_grp_words = x_grp[:].bitcast(F32).rearrange("k (c f) -> k c f", f=8)
+        for bank in range(2):
+            x_t = psum_x.tile([P, 4, P], F32)
+            for s in range(2):
+                for v in range(2):
+                    nc.tensor.transpose(x_t[:, 2 * s + v, :], x_words[:, 2 * bank + s, :, v], sort_pixels[:])
+            nc.vector.tensor_copy(
+                out=x_grp_words[:, :, 4 * bank : 4 * bank + 4], in_=x_t[:].rearrange("k f c -> k c f")
+            )
+        x_codes = keep.tile([P, 4 * ROWS1], U32, align_bytes=64)
+        x_scales = keep.tile([P, 4 * ROWS1], U8, align_bytes=64)
+        nc.vector.quantize_mx(out=x_codes[:].bitcast(FP8X4), scales=x_scales[:], in_=x_grp[:])
+
+        fc_grp = keep.tile([P, GRID1, GRID1, C_MID * PACK], BF16, align_bytes=64)
+        fc_codes = keep.tile([P, GRID1, GRID1 * C_MID], U32, align_bytes=64)
+        fc_scales = keep.tile([P, GRID1, GRID1 * C_MID], U8, align_bytes=64)
+        gc_grp = keep.tile([P, GRID1, 16, C_OUT * PACK], BF16, align_bytes=64)
+        gc_codes = keep.tile([P, GRID1, 16 * C_OUT], U32, align_bytes=64)
+        gc_scales = keep.tile([P, GRID1, 16 * C_OUT], U8, align_bytes=64)
+        h_grp = keep.tile([P, GRID1, GRID1 * ROWS2 * PACK], BF16, align_bytes=64)
+        h_codes = keep.tile([P, GRID1, GRID1 * ROWS2], U32, align_bytes=64)
+        h_scales = keep.tile([P, GRID1, GRID1 * ROWS2], U8, align_bytes=64)
+        o_out = keep.tile([P, GRID1, 2, 2, C_OUT], F32)
+
+        def regroup_child(i):
+            for j in range(GRID1):
+                copy = nc.vector.tensor_copy if j == 0 else nc.scalar.copy
+                copy(
+                    out=fc_grp[:, i, j].rearrange("k (l h r) -> k h r l", l=PACK, r=PACK),
+                    in_=fc_raw[:, i, j].rearrange("k (r h l) -> k h r l", r=PACK, l=PACK),
+                )
+
+        def regroup_gchild(i):
+            nc.vector.tensor_copy(
+                out=gc_grp[:, i, 0:4].rearrange("k g (c s r) -> k g c r s", s=4, r=PACK),
+                in_=gc_raw[:, i, 0:4].rearrange("k g (r c s) -> k g c r s", r=PACK, s=4),
+            )
+            nc.scalar.copy(
+                out=gc_grp[:, i, 4:16].rearrange("k g (o r) -> k g o r", r=PACK),
+                in_=gc_raw[:, i, 4:16].rearrange("k g (r o) -> k g o r", r=PACK),
+            )
+
+        def quantise(codes, scales, grouped):
+            nc.vector.quantize_mx(out=codes.bitcast(FP8X4), scales=scales, in_=grouped)
+
+        def level1(i):
+            h_ps = psum_h.tile([P, GRID1 * C_MID], F32)
+            for v in range(2):
+                g = 2 * (i // 2) + v
+                cols = slice(v * 2 * C_MID, (v + 1) * 2 * C_MID)
+                nc.tensor.matmul_mx(
+                    out=h_ps[:, cols],
+                    lhsT=x_codes[:, g * ROWS1 : (g + 1) * ROWS1].bitcast(FP8X4),
+                    lhsT_scale=x_scales[:, g * ROWS1 : (g + 1) * ROWS1],
+                    rhs=fc_codes[:, i, cols].bitcast(FP8X4),
+                    rhs_scale=fc_scales[:, i, cols],
+                    start=True,
+                    stop=True,
+                )
+            h_t = work.tile([P, GRID1 * C_MID], F32, align_bytes=64)
+            nc.vector.transpose(out=h_t[:], in_=h_ps[:])
+            h_sum = work.tile([P, GRID1 * ROWS2 * PACK], F32)
+            nc.vector.tensor_tensor(
+                out=h_sum[:].rearrange("k (j w l) -> k j w l", j=GRID1, l=PACK),
+                in0=h_t[:].rearrange("k (j l w) -> k j w l", j=GRID1, l=PACK),
+                in1=bias_c[:, i * 16 : (i + 1) * 16]
+                .rearrange("k (j l) -> k j l", l=PACK)
+                .unsqueeze(2)
+                .to_broadcast([P, GRID1, ROWS2, PACK]),
+                op=ADD,
+            )
+            nc.scalar.activation(out=h_grp[:, i], in_=h_sum[:], func=RELU)
+            quantise(h_codes[:, i], h_scales[:, i], h_grp[:, i])
+
+        def level2(i):
+            o_ps = psum_o.tile([P, 16 * C_OUT], F32)
+            nc.tensor.matmul_mx(
+                out=o_ps[:],
+                lhsT=h_codes[:, i].bitcast(FP8X4),
+                lhsT_scale=h_scales[:, i],
+                rhs=gc_codes[:, i].bitcast(FP8X4),
+                rhs_scale=gc_scales[:, i],
+                start=True,
+                stop=True,
+            )
+            o_sum = work.tile([P, 2, 2 * C_OUT], F32)
+            for j in range(GRID1):
+                rows = slice(j * ROWS2, (j + 1) * ROWS2)
+                nc.vector.tensor_tensor(
+                    out=o_sum[rows],
+                    in0=o_ps[rows].rearrange("w (a j f) -> w a j f", a=2, j=GRID1)[:, :, j, :],
+                    in1=bias_g[rows, i * 128 : (i + 1) * 128].rearrange("w (a f) -> w a f", a=2),
+                    op=ADD,
+                )
+            nc.scalar.activation(
+                out=o_out[:, i].rearrange("k a e o -> k (a e o)"),
+                in_=o_sum[:].rearrange("k a f -> k (a f)"),
+                func=RELU,
+            )
+            for j in range(GRID1):
+                rows = slice(j * ROWS2, (j + 1) * ROWS2)
+                for a in range(2):
+                    queue = nc.sync if a == 0 else nc.scalar
+                    queue.dma_start(
+                        out=out[2 * i + a, 2 * j : 2 * j + 2].rearrange("e n y x o -> (n y x) e o"),
+                        in_=o_out[rows, i, a],
+                    )
+
+        regroup_child(0)
+        for i in range(GRID1):
+            if i + 1 < GRID1:
+                regroup_child(i + 1)
+            else:
+                regroup_gchild(0)
+            quantise(fc_codes[:, i], fc_scales[:, i], fc_grp[:, i].rearrange("k j c -> k (j c)"))
+            level1(i)
+        for i in range(GRID1):
+            if i + 1 < GRID1:
+                regroup_gchild(i + 1)
+            quantise(gc_codes[:, i], gc_scales[:, i], gc_grp[:, i].rearrange("k g c -> k (g c)"))
+            level2(i)

@@ -29,53 +29,61 @@ def tile_butterflylayer2d_pa_s_kernel(tc, x_parent, f_child, b_child, f_gchild, 
     with ExitStack() as ctx:
         keep = ctx.enter_context(tc.tile_pool(name="keep", bufs=1))
         work = ctx.enter_context(tc.tile_pool(name="work", bufs=2))
-        psum_prep = ctx.enter_context(tc.psum_pool(name="psum_prep", bufs=1))
-        psum_x = ctx.enter_context(tc.psum_pool(name="psum_x", bufs=2))
+        psum_early = ctx.enter_context(tc.psum_pool(name="psum_early", bufs=2))
         psum_h = ctx.enter_context(tc.psum_pool(name="psum_h", bufs=2))
         psum_o = ctx.enter_context(tc.psum_pool(name="psum_o", bufs=2))
+        psum_t = ctx.enter_context(tc.psum_pool(name="psum_t", bufs=2))
+        ctx.enter_context(tc.manual_schedule())
 
+        fc_raw = keep.tile([P, GRID1, GRID1, PACK * C_MID], BF16)
+        gc_raw = keep.tile([P, GRID1, 2, 8, PACK * C_OUT], BF16)
+
+        def load_child(i):
+            for half in range(2):
+                nodes = slice(2 * half, 2 * half + 2)
+                nc.sync.dma_start(
+                    out=fc_raw[:, i, nodes],
+                    in_=f_child[i, nodes].rearrange("j p q (h l) o -> (p q h) j (l o)", l=PACK),
+                )
+
+        def load_gchild(i):
+            for a in range(2):
+                nc.sync.dma_start(
+                    out=gc_raw[:, i, a],
+                    in_=f_gchild[2 * i + a].rearrange("j p q (h l) o -> (p q h) j (l o)", l=PACK),
+                )
+
+        load_child(0)
         x_rows = keep.tile([P, 4, K], BF16)
         patches = x_parent.rearrange("u v n (y p) (s d q) c -> d p (u v n y) s (q c)", p=2, s=4, d=2)
         for d in range(2):
             for p in range(2):
                 nc.sync.dma_start(out=x_rows[d:P:2, :, p * 256 : (p + 1) * 256], in_=patches[d, p])
-
-        fc_raw = keep.tile([P, GRID1, GRID1, PACK * C_MID], BF16)
-        for i in range(GRID1):
-            nc.sync.dma_start(
-                out=fc_raw[:, i], in_=f_child[i].rearrange("j p q (h l) o -> (p q h) j (l o)", l=PACK)
-            )
-        gc_raw = keep.tile([P, GRID1, 16, PACK * C_OUT], BF16)
-        for i in range(GRID1):
-            nc.sync.dma_start(
-                out=gc_raw[:, i],
-                in_=f_gchild[2 * i : 2 * i + 2].rearrange("a j p q (h l) o -> (p q h) (a j) (l o)", l=PACK),
-            )
-
         bc_rows = keep.tile([P, 16 * PACK], BF16)
         nc.vector.memset(bc_rows[:], 0.0)
-        nc.scalar.dma_start(
+        nc.sync.dma_start(
             out=bc_rows[0:HI, :].rearrange("h (n l) -> h n l", l=PACK),
             in_=b_child.rearrange("i j (h l) -> h (i j) l", l=PACK),
         )
-        bg_rows = keep.tile([P, 8 * 2 * C_OUT], BF16)
+        bg_rows = keep.tile([P, GRID1 * P], BF16)
         nc.vector.memset(bg_rows[:], 0.0)
-        nc.scalar.dma_start(
+        nc.sync.dma_start(
             out=bg_rows[0:GRID1, :].rearrange("j (i f) -> j i f", i=8),
             in_=b_gchild.rearrange("i (j e) o -> j i (e o)", e=2),
         )
+        for i in range(1, GRID1):
+            load_child(i)
+        for i in range(GRID1):
+            load_gchild(i)
 
         ident = keep.tile([P, P], F32)
         make_identity(nc, ident[:])
+        ident_bf = keep.tile([P, P], BF16)
+        nc.vector.tensor_copy(out=ident_bf[:], in_=ident[:])
         spread_c = keep.tile([P, P], BF16)
         nc.vector.tensor_copy(
             out=spread_c[:].rearrange("k (t h) -> k t h", t=4),
             in_=ident[:, 0:HI].unsqueeze(1).to_broadcast([P, 4, HI]),
-        )
-        spread_g = keep.tile([P, P], BF16)
-        nc.vector.tensor_copy(
-            out=spread_g[:].rearrange("k (j w) -> k j w", j=GRID1),
-            in_=ident[:, 0:GRID1].unsqueeze(2).to_broadcast([P, GRID1, ROWS2]),
         )
         sort_pixels = keep.tile([P, P], F32)
         nc.vector.tensor_copy(
@@ -83,135 +91,166 @@ def tile_butterflylayer2d_pa_s_kernel(tc, x_parent, f_child, b_child, f_gchild, 
             in_=ident[:].rearrange("r (g a t) -> r g t a", g=4, t=4),
         )
 
-        bc_ps = psum_prep.tile([P, 16 * PACK], F32)
-        nc.tensor.matmul(out=bc_ps[:], lhsT=spread_c[:], rhs=bc_rows[:], start=True, stop=True)
-        bias_c = keep.tile([P, 16 * PACK], F32)
-        nc.vector.tensor_copy(out=bias_c[:], in_=bc_ps[:])
-        bg_ps = psum_prep.tile([P, 8 * 2 * C_OUT], F32)
-        nc.tensor.matmul(out=bg_ps[:], lhsT=spread_g[:], rhs=bg_rows[:], start=True, stop=True)
-        bias_g = keep.tile([P, 8 * 2 * C_OUT], F32)
-        nc.scalar.copy(out=bias_g[:], in_=bg_ps[:])
-
-        x_words = x_rows[:].bitcast(F32).rearrange("c s (k v) -> c s k v", v=2)
         x_grp = keep.tile([P, 4 * ROWS1 * PACK], BF16, align_bytes=64)
-        x_grp_words = x_grp[:].bitcast(F32).rearrange("k (c f) -> k c f", f=8)
-        for bank in range(2):
-            x_t = psum_x.tile([P, 4, P], F32)
-            for s in range(2):
-                for v in range(2):
-                    nc.tensor.transpose(x_t[:, 2 * s + v, :], x_words[:, 2 * bank + s, :, v], sort_pixels[:])
-            nc.vector.tensor_copy(
-                out=x_grp_words[:, :, 4 * bank : 4 * bank + 4], in_=x_t[:].rearrange("k f c -> k c f")
-            )
         x_codes = keep.tile([P, 4 * ROWS1], U32, align_bytes=64)
         x_scales = keep.tile([P, 4 * ROWS1], U8, align_bytes=64)
-        nc.vector.quantize_mx(out=x_codes[:].bitcast(FP8X4), scales=x_scales[:], in_=x_grp[:])
+        bias_c = keep.tile([P, 16 * PACK], F32)
+        bias_g = keep.tile([P, GRID1, GRID1], F32)
+
+        def prepare_x():
+            x_words = x_rows[:].bitcast(F32).rearrange("c s (k v) -> c s k v", v=2)
+            x_grp_words = x_grp[:].bitcast(F32).rearrange("k (c f) -> k c f", f=8)
+            for bank in range(2):
+                x_t = psum_early.tile([P, 4, P], F32, tag="early")
+                for s in range(2):
+                    for v in range(2):
+                        nc.tensor.transpose(x_t[:, 2 * s + v, :], x_words[:, 2 * bank + s, :, v], sort_pixels[:])
+                nc.vector.tensor_copy(
+                    out=x_grp_words[:, :, 4 * bank : 4 * bank + 4], in_=x_t[:].rearrange("k f c -> k c f")
+                )
+            nc.vector.quantize_mx(out=x_codes[:].bitcast(FP8X4), scales=x_scales[:], in_=x_grp[:])
+
+        def prepare_biases():
+            bc_ps = psum_early.tile([P, 16 * PACK], F32, tag="early")
+            nc.tensor.matmul(out=bc_ps[:], lhsT=spread_c[:], rhs=bc_rows[:], start=True, stop=True)
+            nc.vector.tensor_copy(out=bias_c[:], in_=bc_ps[:])
+            bg_ps = psum_early.tile([P, GRID1, P], BF16, tag="early")
+            for i in range(GRID1):
+                nc.tensor.transpose(bg_ps[:, i, :], bg_rows[:, i * P : (i + 1) * P], ident_bf[:])
+            nc.vector.tensor_copy(out=bias_g[:], in_=bg_ps[:, :, 0:GRID1])
 
         fc_grp = keep.tile([P, GRID1, GRID1, C_MID * PACK], BF16, align_bytes=64)
         fc_codes = keep.tile([P, GRID1, GRID1 * C_MID], U32, align_bytes=64)
         fc_scales = keep.tile([P, GRID1, GRID1 * C_MID], U8, align_bytes=64)
-        gc_grp = keep.tile([P, GRID1, 16, C_OUT * PACK], BF16, align_bytes=64)
-        gc_codes = keep.tile([P, GRID1, 16 * C_OUT], U32, align_bytes=64)
-        gc_scales = keep.tile([P, GRID1, 16 * C_OUT], U8, align_bytes=64)
+        gc_grp = keep.tile([P, GRID1, GRID1, 2, 2, C_OUT * PACK], BF16, align_bytes=64)
+        gc_codes = keep.tile([P, GRID1, GRID1 * P], U32, align_bytes=64)
+        gc_scales = keep.tile([P, GRID1, GRID1 * P], U8, align_bytes=64)
         h_grp = keep.tile([P, GRID1, GRID1 * ROWS2 * PACK], BF16, align_bytes=64)
         h_codes = keep.tile([P, GRID1, GRID1 * ROWS2], U32, align_bytes=64)
         h_scales = keep.tile([P, GRID1, GRID1 * ROWS2], U8, align_bytes=64)
         o_out = keep.tile([P, GRID1, 2, 2, C_OUT], F32)
+        banks = {}
 
-        def regroup_child(i):
-            for j in range(GRID1):
-                copy = nc.vector.tensor_copy if j == 0 else nc.scalar.copy
-                copy(
-                    out=fc_grp[:, i, j].rearrange("k (l h r) -> k h r l", l=PACK, r=PACK),
-                    in_=fc_raw[:, i, j].rearrange("k (r h l) -> k h r l", r=PACK, l=PACK),
-                )
-
-        def regroup_gchild(i):
-            nc.vector.tensor_copy(
-                out=gc_grp[:, i, 0:4].rearrange("k g (c s r) -> k g c r s", s=4, r=PACK),
-                in_=gc_raw[:, i, 0:4].rearrange("k g (r c s) -> k g c r s", r=PACK, s=4),
-            )
-            nc.scalar.copy(
-                out=gc_grp[:, i, 4:16].rearrange("k g (o r) -> k g o r", r=PACK),
-                in_=gc_raw[:, i, 4:16].rearrange("k g (r o) -> k g o r", r=PACK),
-            )
-
-        def quantise(codes, scales, grouped):
-            nc.vector.quantize_mx(out=codes.bitcast(FP8X4), scales=scales, in_=grouped)
-
-        def level1(i):
-            h_ps = psum_h.tile([P, GRID1 * C_MID], F32)
-            for v in range(2):
-                g = 2 * (i // 2) + v
-                cols = slice(v * 2 * C_MID, (v + 1) * 2 * C_MID)
-                nc.tensor.matmul_mx(
-                    out=h_ps[:, cols],
-                    lhsT=x_codes[:, g * ROWS1 : (g + 1) * ROWS1].bitcast(FP8X4),
-                    lhsT_scale=x_scales[:, g * ROWS1 : (g + 1) * ROWS1],
-                    rhs=fc_codes[:, i, cols].bitcast(FP8X4),
-                    rhs_scale=fc_scales[:, i, cols],
-                    start=True,
-                    stop=True,
-                )
-            h_t = work.tile([P, GRID1 * C_MID], F32, align_bytes=64)
-            nc.vector.transpose(out=h_t[:], in_=h_ps[:])
-            h_sum = work.tile([P, GRID1 * ROWS2 * PACK], F32)
-            nc.vector.tensor_tensor(
-                out=h_sum[:].rearrange("k (j w l) -> k j w l", j=GRID1, l=PACK),
-                in0=h_t[:].rearrange("k (j l w) -> k j w l", j=GRID1, l=PACK),
-                in1=bias_c[:, i * 16 : (i + 1) * 16]
-                .rearrange("k (j l) -> k j l", l=PACK)
-                .unsqueeze(2)
-                .to_broadcast([P, GRID1, ROWS2, PACK]),
-                op=ADD,
-            )
-            nc.scalar.activation(out=h_grp[:, i], in_=h_sum[:], func=RELU)
-            quantise(h_codes[:, i], h_scales[:, i], h_grp[:, i])
-
-        def level2(i):
-            o_ps = psum_o.tile([P, 16 * C_OUT], F32)
-            nc.tensor.matmul_mx(
-                out=o_ps[:],
-                lhsT=h_codes[:, i].bitcast(FP8X4),
-                lhsT_scale=h_scales[:, i],
-                rhs=gc_codes[:, i].bitcast(FP8X4),
-                rhs_scale=gc_scales[:, i],
-                start=True,
-                stop=True,
-            )
-            o_sum = work.tile([P, 2, 2 * C_OUT], F32)
-            for j in range(GRID1):
-                rows = slice(j * ROWS2, (j + 1) * ROWS2)
-                nc.vector.tensor_tensor(
-                    out=o_sum[rows],
-                    in0=o_ps[rows].rearrange("w (a j f) -> w a j f", a=2, j=GRID1)[:, :, j, :],
-                    in1=bias_g[rows, i * 128 : (i + 1) * 128].rearrange("w (a f) -> w a f", a=2),
-                    op=ADD,
-                )
-            nc.scalar.activation(
-                out=o_out[:, i].rearrange("k a e o -> k (a e o)"),
-                in_=o_sum[:].rearrange("k a f -> k (a f)"),
-                func=RELU,
-            )
-            for j in range(GRID1):
-                rows = slice(j * ROWS2, (j + 1) * ROWS2)
+        def regroup(c):
+            i = c % GRID1
+            if c < GRID1:
+                for j in range(GRID1):
+                    copy = nc.vector.tensor_copy if j == 0 else nc.scalar.copy
+                    copy(
+                        out=fc_grp[:, i, j].rearrange("k (l h r) -> k h r l", l=PACK, r=PACK),
+                        in_=fc_raw[:, i, j].rearrange("k (r h l) -> k h r l", r=PACK, l=PACK),
+                    )
+            else:
                 for a in range(2):
-                    queue = nc.sync if a == 0 else nc.scalar
-                    queue.dma_start(
-                        out=out[2 * i + a, 2 * j : 2 * j + 2].rearrange("e n y x o -> (n y x) e o"),
-                        in_=o_out[rows, i, a],
+                    copy = nc.scalar.copy if a == 0 else nc.vector.tensor_copy
+                    copy(
+                        out=gc_grp[:, i, :, a].rearrange("k j e (o r) -> k j e o r", r=PACK),
+                        in_=gc_raw[:, i, a].rearrange("k (j e) (r o) -> k j e o r", e=2, r=PACK),
                     )
 
-        regroup_child(0)
-        for i in range(GRID1):
-            if i + 1 < GRID1:
-                regroup_child(i + 1)
+        def quantise_weights(c):
+            i = c % GRID1
+            if c < GRID1:
+                codes, scales, grouped = fc_codes, fc_scales, fc_grp[:, i].rearrange("k j c -> k (j c)")
             else:
-                regroup_gchild(0)
-            quantise(fc_codes[:, i], fc_scales[:, i], fc_grp[:, i].rearrange("k j c -> k (j c)"))
-            level1(i)
-        for i in range(GRID1):
-            if i + 1 < GRID1:
-                regroup_gchild(i + 1)
-            quantise(gc_codes[:, i], gc_scales[:, i], gc_grp[:, i].rearrange("k g c -> k (g c)"))
-            level2(i)
+                codes, scales, grouped = gc_codes, gc_scales, gc_grp[:, i].rearrange("k j a e c -> k (j a e c)")
+            nc.vector.quantize_mx(out=codes[:, i].bitcast(FP8X4), scales=scales[:, i], in_=grouped)
+
+        def multiply(c):
+            i = c % GRID1
+            if c < GRID1:
+                h_ps = psum_h.tile([P, GRID1 * C_MID], F32)
+                for v in range(2):
+                    g = 2 * (i // 2) + v
+                    cols = slice(v * 2 * C_MID, (v + 1) * 2 * C_MID)
+                    nc.tensor.matmul_mx(
+                        out=h_ps[:, cols],
+                        lhsT=x_codes[:, g * ROWS1 : (g + 1) * ROWS1].bitcast(FP8X4),
+                        lhsT_scale=x_scales[:, g * ROWS1 : (g + 1) * ROWS1],
+                        rhs=fc_codes[:, i, cols].bitcast(FP8X4),
+                        rhs_scale=fc_scales[:, i, cols],
+                        start=True,
+                        stop=True,
+                    )
+                banks[c] = h_ps
+            else:
+                o_ps = psum_o.tile([P, GRID1 * P], F32)
+                for j in range(GRID1):
+                    cols = slice(j * P, (j + 1) * P)
+                    nc.tensor.matmul_mx(
+                        out=o_ps[:, cols],
+                        lhsT=gc_codes[:, i, cols].bitcast(FP8X4),
+                        lhsT_scale=gc_scales[:, i, cols],
+                        rhs=h_codes[:, i].bitcast(FP8X4),
+                        rhs_scale=h_scales[:, i],
+                        start=True,
+                        stop=True,
+                    )
+                banks[c] = o_ps
+
+        def turn(c):
+            i = c % GRID1
+            if c < GRID1:
+                h_t = work.tile([P, GRID1 * C_MID], F32, align_bytes=64)
+                nc.vector.transpose(out=h_t[:], in_=banks[c][:])
+                if c >= 1:
+                    quantise_h(c - 1)
+                h_sum = work.tile([P, GRID1 * ROWS2 * PACK], F32)
+                nc.vector.tensor_tensor(
+                    out=h_sum[:].rearrange("k (j w l) -> k j w l", j=GRID1, l=PACK),
+                    in0=h_t[:].rearrange("k (j l w) -> k j w l", j=GRID1, l=PACK),
+                    in1=bias_c[:, i * 16 : (i + 1) * 16]
+                    .rearrange("k (j l) -> k j l", l=PACK)
+                    .unsqueeze(2)
+                    .to_broadcast([P, GRID1, ROWS2, PACK]),
+                    op=ADD,
+                )
+                banks[c] = h_sum
+            else:
+                if c == GRID1:
+                    quantise_h(c - 1)
+                o_sum = work.tile([P, GRID1, ROWS2], F32)
+                nc.vector.tensor_tensor(
+                    out=o_sum[:],
+                    in0=banks[c][:].rearrange("m (x w) -> m x w", w=ROWS2)[:, 0 : GRID1 * GRID1 : GRID1 + 1, :],
+                    in1=bias_g[:, i, :].unsqueeze(2).to_broadcast([P, GRID1, ROWS2]),
+                    op=ADD,
+                )
+                o_t = psum_t.tile([P, P], F32)
+                nc.tensor.transpose(o_t[:], o_sum[:].rearrange("m j w -> m (j w)"), ident[:])
+                banks[c] = o_t
+
+        def quantise_h(c):
+            nc.vector.quantize_mx(out=h_codes[:, c].bitcast(FP8X4), scales=h_scales[:, c], in_=h_grp[:, c])
+
+        def finish(c):
+            i = c % GRID1
+            if c < GRID1:
+                nc.scalar.activation(out=h_grp[:, i], in_=banks[c][:], func=RELU)
+            else:
+                nc.scalar.activation(out=o_out[:, i].rearrange("k a e o -> k (a e o)"), in_=banks[c][:], func=RELU)
+                for j in range(GRID1):
+                    for a in range(2):
+                        nc.sync.dma_start(
+                            out=out[2 * i + a, 2 * j : 2 * j + 2].rearrange("e n y x o -> (n y x) e o"),
+                            in_=o_out[j * ROWS2 : (j + 1) * ROWS2, i, a],
+                        )
+
+        chunks = 2 * GRID1
+
+        def run(stage, c):
+            if 0 <= c < chunks:
+                stage(c)
+
+        regroup(0)
+        quantise_weights(0)
+        regroup(1)
+        prepare_x()
+        prepare_biases()
+        multiply(0)
+        for n in range(2, chunks + 3):
+            run(finish, n - 3)
+            run(quantise_weights, n - 1)
+            run(regroup, n)
+            run(multiply, n - 1)
+            run(turn, n - 2)

@@ -48,10 +48,12 @@ def tile_butterflylayer2d_pa_s_kernel(tc, x_parent, f_child, b_child, f_gchild, 
 
         def load_gchild(i):
             for a in range(2):
-                nc.sync.dma_start(
-                    out=gc_raw[:, i, a],
-                    in_=f_gchild[2 * i + a].rearrange("j p q (h l) o -> (p q h) j (l o)", l=PACK),
-                )
+                for half in range(2):
+                    nodes = slice(4 * half, 4 * half + 4)
+                    nc.sync.dma_start(
+                        out=gc_raw[:, i, a, nodes],
+                        in_=f_gchild[2 * i + a, nodes].rearrange("j p q (h l) o -> (p q h) j (l o)", l=PACK),
+                    )
 
         load_child(0)
         x_rows = keep.tile([P, 4, K], BF16)

@@ -21,6 +21,8 @@ ROWS1 = 128
 ROWS2 = 32
 HI = C_MID // PACK
 
+VECTOR_UNITS = ((0, 2), (0, 2), (0, 1), (0, 1), (2,), (2, 3), (2,), (2, 3))
+
 FLOPS = 2 * 16 * ROWS1 * K * C_MID + 2 * 64 * ROWS2 * K * C_OUT
 
 
@@ -38,12 +40,11 @@ def tile_butterflylayer2d_pa_s_kernel(tc, x_parent, f_child, b_child, f_gchild, 
         fc_raw = keep.tile([P, GRID1, GRID1, PACK * C_MID], BF16)
         gc_raw = keep.tile([P, GRID1, 2, 8, PACK * C_OUT], BF16)
 
-        def load_child(i):
-            for half in range(2):
-                nodes = slice(2 * half, 2 * half + 2)
+        def load_child(i, width):
+            for j in range(0, GRID1, width):
                 nc.sync.dma_start(
-                    out=fc_raw[:, i, nodes],
-                    in_=f_child[i, nodes].rearrange("j p q (h l) o -> (p q h) j (l o)", l=PACK),
+                    out=fc_raw[:, i, j : j + width],
+                    in_=f_child[i, j : j + width].rearrange("j p q (h l) o -> (p q h) j (l o)", l=PACK),
                 )
 
         def load_gchild(i):
@@ -55,26 +56,22 @@ def tile_butterflylayer2d_pa_s_kernel(tc, x_parent, f_child, b_child, f_gchild, 
                         in_=f_gchild[2 * i + a, nodes].rearrange("j p q (h l) o -> (p q h) j (l o)", l=PACK),
                     )
 
-        load_child(0)
+        load_child(0, 1)
+        load_child(1, 2)
+        b_rows = keep.tile([P, GRID1 + 1, P], BF16)
+        nc.vector.memset(b_rows[:], 0.0)
+        nc.sync.dma_start(out=b_rows[0:16, GRID1, :], in_=b_child.rearrange("i j c -> (i j) c"))
+        nc.sync.dma_start(
+            out=b_rows[0:GRID1, 0:GRID1, :].rearrange("j i (a f) -> j (i a) f", a=2),
+            in_=b_gchild.rearrange("i (j e) o -> j i (e o)", e=2),
+        )
         x_rows = keep.tile([P, 4, K], BF16)
         patches = x_parent.rearrange("u v n (y p) (s d q) c -> d p (u v n y) s (q c)", p=2, s=4, d=2)
         for d in range(2):
             for p in range(2):
                 nc.sync.dma_start(out=x_rows[d:P:2, :, p * 256 : (p + 1) * 256], in_=patches[d, p])
-        bc_rows = keep.tile([P, 16 * PACK], BF16)
-        nc.vector.memset(bc_rows[:], 0.0)
-        nc.sync.dma_start(
-            out=bc_rows[0:HI, :].rearrange("h (n l) -> h n l", l=PACK),
-            in_=b_child.rearrange("i j (h l) -> h (i j) l", l=PACK),
-        )
-        bg_rows = keep.tile([P, GRID1 * P], BF16)
-        nc.vector.memset(bg_rows[:], 0.0)
-        nc.sync.dma_start(
-            out=bg_rows[0:GRID1, :].rearrange("j (i f) -> j i f", i=8),
-            in_=b_gchild.rearrange("i (j e) o -> j i (e o)", e=2),
-        )
-        for i in range(1, GRID1):
-            load_child(i)
+        for i in range(2, GRID1):
+            load_child(i, 2)
         for i in range(GRID1):
             load_gchild(i)
 
@@ -82,10 +79,10 @@ def tile_butterflylayer2d_pa_s_kernel(tc, x_parent, f_child, b_child, f_gchild, 
         make_identity(nc, ident[:])
         ident_bf = keep.tile([P, P], BF16)
         nc.vector.tensor_copy(out=ident_bf[:], in_=ident[:])
-        spread_c = keep.tile([P, P], BF16)
+        sort_channels = keep.tile([P, P], BF16)
         nc.vector.tensor_copy(
-            out=spread_c[:].rearrange("k (t h) -> k t h", t=4),
-            in_=ident[:, 0:HI].unsqueeze(1).to_broadcast([P, 4, HI]),
+            out=sort_channels[:].rearrange("c (v h s) -> c v h s", v=2, s=2),
+            in_=ident[:].rearrange("c (h v s) -> c v h s", v=2, s=2),
         )
         sort_pixels = keep.tile([P, P], F32)
         nc.vector.tensor_copy(
@@ -96,30 +93,28 @@ def tile_butterflylayer2d_pa_s_kernel(tc, x_parent, f_child, b_child, f_gchild, 
         x_grp = keep.tile([P, 4 * ROWS1 * PACK], BF16, align_bytes=64)
         x_codes = keep.tile([P, 4 * ROWS1], U32, align_bytes=64)
         x_scales = keep.tile([P, 4 * ROWS1], U8, align_bytes=64)
-        bias_c = keep.tile([P, 16 * PACK], F32)
-        bias_g = keep.tile([P, GRID1, GRID1], F32)
+        bias = keep.tile([P, GRID1 + 1, 16], F32)
 
-        def prepare_x():
+        def transpose_x():
             x_words = x_rows[:].bitcast(F32).rearrange("c s (k v) -> c s k v", v=2)
-            x_grp_words = x_grp[:].bitcast(F32).rearrange("k (c f) -> k c f", f=8)
+            tiles = []
             for bank in range(2):
                 x_t = psum_early.tile([P, 4, P], F32, tag="early")
                 for s in range(2):
                     for v in range(2):
                         nc.tensor.transpose(x_t[:, 2 * s + v, :], x_words[:, 2 * bank + s, :, v], sort_pixels[:])
-                nc.vector.tensor_copy(
-                    out=x_grp_words[:, :, 4 * bank : 4 * bank + 4], in_=x_t[:].rearrange("k f c -> k c f")
-                )
-            nc.vector.quantize_mx(out=x_codes[:].bitcast(FP8X4), scales=x_scales[:], in_=x_grp[:])
+                tiles.append(x_t)
+            return tiles
 
-        def prepare_biases():
-            bc_ps = psum_early.tile([P, 16 * PACK], F32, tag="early")
-            nc.tensor.matmul(out=bc_ps[:], lhsT=spread_c[:], rhs=bc_rows[:], start=True, stop=True)
-            nc.vector.tensor_copy(out=bias_c[:], in_=bc_ps[:])
-            bg_ps = psum_early.tile([P, GRID1, P], BF16, tag="early")
-            for i in range(GRID1):
-                nc.tensor.transpose(bg_ps[:, i, :], bg_rows[:, i * P : (i + 1) * P], ident_bf[:])
-            nc.vector.tensor_copy(out=bias_g[:], in_=bg_ps[:, :, 0:GRID1])
+        def group_x(copy, bank, x_t):
+            x_grp_words = x_grp[:].bitcast(F32).rearrange("k (c f) -> k c f", f=8)
+            copy(out=x_grp_words[:, :, 4 * bank : 4 * bank + 4], in_=x_t[:].rearrange("k f c -> k c f"))
+
+        def transpose_biases():
+            b_ps = psum_h.tile([P, GRID1 + 1, P], BF16, tag="h")
+            for i in range(GRID1 + 1):
+                nc.tensor.transpose(b_ps[:, i, :], b_rows[:, i, :], ident_bf[:])
+            return b_ps
 
         fc_grp = keep.tile([P, GRID1, GRID1, C_MID * PACK], BF16, align_bytes=64)
         fc_codes = keep.tile([P, GRID1, GRID1 * C_MID], U32, align_bytes=64)
@@ -127,28 +122,33 @@ def tile_butterflylayer2d_pa_s_kernel(tc, x_parent, f_child, b_child, f_gchild, 
         gc_grp = keep.tile([P, GRID1, GRID1, 2, 2, C_OUT * PACK], BF16, align_bytes=64)
         gc_codes = keep.tile([P, GRID1, GRID1 * P], U32, align_bytes=64)
         gc_scales = keep.tile([P, GRID1, GRID1 * P], U8, align_bytes=64)
+        h_rows = keep.tile([P, GRID1, GRID1, ROWS1], BF16)
         h_grp = keep.tile([P, GRID1, GRID1 * ROWS2 * PACK], BF16, align_bytes=64)
         h_codes = keep.tile([P, GRID1, GRID1 * ROWS2], U32, align_bytes=64)
         h_scales = keep.tile([P, GRID1, GRID1 * ROWS2], U8, align_bytes=64)
         o_out = keep.tile([P, GRID1, 2, 2, C_OUT], F32)
         banks = {}
 
-        def regroup(c):
+        def regroup(copy, c, units):
             i = c % GRID1
-            if c < GRID1:
-                for j in range(GRID1):
-                    copy = nc.vector.tensor_copy if j == 0 else nc.scalar.copy
+            for unit in units:
+                if c < GRID1:
                     copy(
-                        out=fc_grp[:, i, j].rearrange("k (l h r) -> k h r l", l=PACK, r=PACK),
-                        in_=fc_raw[:, i, j].rearrange("k (r h l) -> k h r l", r=PACK, l=PACK),
+                        out=fc_grp[:, i, unit].rearrange("k (h m r) -> k h r m", m=4, r=PACK),
+                        in_=fc_raw[:, i, unit].rearrange("k (r h m) -> k h r m", r=PACK, m=4),
                     )
-            else:
-                for a in range(2):
-                    copy = nc.scalar.copy if a == 0 else nc.vector.tensor_copy
+                else:
+                    a, e = divmod(unit, 2)
                     copy(
-                        out=gc_grp[:, i, :, a].rearrange("k j e (o r) -> k j e o r", r=PACK),
-                        in_=gc_raw[:, i, a].rearrange("k (j e) (r o) -> k j e o r", e=2, r=PACK),
+                        out=gc_grp[:, i, :, a, e].rearrange("k j (h m r) -> k j h r m", m=4, r=PACK),
+                        in_=gc_raw[:, i, a, e : 8 : 2].rearrange("k j (r h m) -> k j h r m", r=PACK, m=4),
                     )
+
+        def regroup_on_scalar(c):
+            regroup(nc.scalar.copy, c, [unit for unit in range(4) if unit not in VECTOR_UNITS[c]])
+
+        def regroup_on_vector(c, units):
+            regroup(nc.vector.tensor_copy, c, units)
 
         def quantise_weights(c):
             i = c % GRID1
@@ -161,16 +161,16 @@ def tile_butterflylayer2d_pa_s_kernel(tc, x_parent, f_child, b_child, f_gchild, 
         def multiply(c):
             i = c % GRID1
             if c < GRID1:
-                h_ps = psum_h.tile([P, GRID1 * C_MID], F32)
-                for v in range(2):
-                    g = 2 * (i // 2) + v
-                    cols = slice(v * 2 * C_MID, (v + 1) * 2 * C_MID)
+                h_ps = psum_h.tile([P, GRID1 * ROWS1], F32, tag="h")
+                for j in range(GRID1):
+                    g = 2 * (i // 2) + j // 2
+                    cols = slice(j * C_MID, (j + 1) * C_MID)
                     nc.tensor.matmul_mx(
-                        out=h_ps[:, cols],
-                        lhsT=x_codes[:, g * ROWS1 : (g + 1) * ROWS1].bitcast(FP8X4),
-                        lhsT_scale=x_scales[:, g * ROWS1 : (g + 1) * ROWS1],
-                        rhs=fc_codes[:, i, cols].bitcast(FP8X4),
-                        rhs_scale=fc_scales[:, i, cols],
+                        out=h_ps[:, j * ROWS1 : (j + 1) * ROWS1],
+                        lhsT=fc_codes[:, i, cols].bitcast(FP8X4),
+                        lhsT_scale=fc_scales[:, i, cols],
+                        rhs=x_codes[:, g * ROWS1 : (g + 1) * ROWS1].bitcast(FP8X4),
+                        rhs_scale=x_scales[:, g * ROWS1 : (g + 1) * ROWS1],
                         start=True,
                         stop=True,
                     )
@@ -190,69 +190,106 @@ def tile_butterflylayer2d_pa_s_kernel(tc, x_parent, f_child, b_child, f_gchild, 
                     )
                 banks[c] = o_ps
 
-        def turn(c):
-            i = c % GRID1
-            if c < GRID1:
-                h_t = work.tile([P, GRID1 * C_MID], F32, align_bytes=64)
-                nc.vector.transpose(out=h_t[:], in_=banks[c][:])
-                if c >= 1:
-                    quantise_h(c - 1)
-                h_sum = work.tile([P, GRID1 * ROWS2 * PACK], F32)
-                nc.vector.tensor_tensor(
-                    out=h_sum[:].rearrange("k (j w l) -> k j w l", j=GRID1, l=PACK),
-                    in0=h_t[:].rearrange("k (j l w) -> k j w l", j=GRID1, l=PACK),
-                    in1=bias_c[:, i * 16 : (i + 1) * 16]
-                    .rearrange("k (j l) -> k j l", l=PACK)
-                    .unsqueeze(2)
-                    .to_broadcast([P, GRID1, ROWS2, PACK]),
-                    op=ADD,
+        def activate_h(i):
+            for j in range(GRID1):
+                nc.scalar.activation(
+                    out=h_rows[:, i, j],
+                    in_=banks[i][:, j * ROWS1 : (j + 1) * ROWS1],
+                    func=RELU,
+                    bias=bias[:, GRID1, GRID1 * i + j : GRID1 * i + j + 1],
                 )
-                banks[c] = h_sum
-            else:
-                if c == GRID1:
-                    quantise_h(c - 1)
-                o_sum = work.tile([P, GRID1, ROWS2], F32)
-                nc.vector.tensor_tensor(
-                    out=o_sum[:],
-                    in0=banks[c][:].rearrange("m (x w) -> m x w", w=ROWS2)[:, 0 : GRID1 * GRID1 : GRID1 + 1, :],
-                    in1=bias_g[:, i, :].unsqueeze(2).to_broadcast([P, GRID1, ROWS2]),
-                    op=ADD,
+
+        def transpose_h(i):
+            h_ps = psum_early.tile([P, GRID1, C_MID], BF16, tag="early")
+            for j in range(GRID1):
+                nc.tensor.transpose(h_ps[:, j, :], h_rows[:, i, j], sort_channels[:])
+            banks[i] = h_ps
+
+        def swap_h(i):
+            h_t = work.tile([P, GRID1 * C_MID // 2], F32, align_bytes=64)
+            for half in range(2):
+                nc.vector.transpose(
+                    out=h_t[:, half * C_MID : (half + 1) * C_MID],
+                    in_=banks[i][:, 2 * half : 2 * half + 2].rearrange("p j c -> p (j c)").bitcast(F32),
                 )
-                o_t = psum_t.tile([P, P], F32)
-                nc.tensor.transpose(o_t[:], o_sum[:].rearrange("m j w -> m (j w)"), ident[:])
-                banks[c] = o_t
+            banks[i] = h_t
+
+        def group_h(i):
+            nc.vector.tensor_copy(
+                out=h_grp[:, i].bitcast(F32).rearrange("k (j w v) -> k j w v", j=GRID1, v=2),
+                in_=banks[i][:].rearrange("k (j v w) -> k j w v", j=GRID1, v=2),
+            )
+
+        def add_bias(i):
+            o_sum = work.tile([P, GRID1, ROWS2], F32)
+            nc.vector.tensor_tensor(
+                out=o_sum[:],
+                in0=banks[GRID1 + i][:].rearrange("m (x w) -> m x w", w=ROWS2)[:, 0 : GRID1 * GRID1 : GRID1 + 1, :],
+                in1=bias[:, i, 0:GRID1].unsqueeze(2).to_broadcast([P, GRID1, ROWS2]),
+                op=ADD,
+            )
+            o_t = psum_t.tile([P, P], F32)
+            nc.tensor.transpose(o_t[:], o_sum[:].rearrange("m j w -> m (j w)"), ident[:])
+            banks[GRID1 + i] = o_t
 
         def quantise_h(c):
             nc.vector.quantize_mx(out=h_codes[:, c].bitcast(FP8X4), scales=h_scales[:, c], in_=h_grp[:, c])
 
-        def finish(c):
-            i = c % GRID1
-            if c < GRID1:
-                nc.scalar.activation(out=h_grp[:, i], in_=banks[c][:], func=RELU)
-            else:
-                nc.scalar.activation(out=o_out[:, i].rearrange("k a e o -> k (a e o)"), in_=banks[c][:], func=RELU)
-                for j in range(GRID1):
-                    for a in range(2):
-                        nc.sync.dma_start(
-                            out=out[2 * i + a, 2 * j : 2 * j + 2].rearrange("e n y x o -> (n y x) e o"),
-                            in_=o_out[j * ROWS2 : (j + 1) * ROWS2, i, a],
-                        )
+        def finish(i):
+            nc.scalar.activation(out=o_out[:, i].rearrange("k a e o -> k (a e o)"), in_=banks[GRID1 + i][:], func=RELU)
+            for j in range(GRID1):
+                for a in range(2):
+                    nc.sync.dma_start(
+                        out=out[2 * i + a, 2 * j : 2 * j + 2].rearrange("e n y x o -> (n y x) e o"),
+                        in_=o_out[j * ROWS2 : (j + 1) * ROWS2, i, a],
+                    )
 
-        chunks = 2 * GRID1
+        def is_child(c):
+            return 0 <= c < GRID1
 
-        def run(stage, c):
-            if 0 <= c < chunks:
-                stage(c)
+        def is_gchild(c):
+            return GRID1 <= c < 2 * GRID1
 
-        regroup(0)
+        regroup_on_scalar(0)
+        regroup_on_vector(0, VECTOR_UNITS[0])
+        regroup_on_scalar(1)
+        regroup_on_vector(1, VECTOR_UNITS[1][:1])
         quantise_weights(0)
-        regroup(1)
-        prepare_x()
-        prepare_biases()
+        regroup_on_vector(1, VECTOR_UNITS[1][1:])
+        b_ps = transpose_biases()
+        x_banks = transpose_x()
+        quantise_weights(1)
+        nc.vector.tensor_copy(out=bias[:], in_=b_ps[:, :, 0:16])
+        regroup_on_vector(2, VECTOR_UNITS[2][:1])
+        group_x(nc.vector.tensor_copy, 0, x_banks[0])
+        group_x(nc.scalar.copy, 1, x_banks[1])
+        regroup_on_vector(2, VECTOR_UNITS[2][1:])
+        nc.vector.quantize_mx(out=x_codes[:].bitcast(FP8X4), scales=x_scales[:], in_=x_grp[:])
+        regroup_on_scalar(2)
         multiply(0)
-        for n in range(2, chunks + 3):
-            run(finish, n - 3)
-            run(quantise_weights, n - 1)
-            run(regroup, n)
-            run(multiply, n - 1)
-            run(turn, n - 2)
+        multiply(1)
+        activate_h(0)
+        transpose_h(0)
+        for n in range(3, 2 * GRID1 + 2):
+            if is_child(n - 2):
+                activate_h(n - 2)
+            if n < 2 * GRID1:
+                regroup_on_scalar(n)
+                regroup_on_vector(n, VECTOR_UNITS[n][:1])
+            if n <= 2 * GRID1:
+                quantise_weights(n - 1)
+                multiply(n - 1)
+            if is_child(n - 2):
+                transpose_h(n - 2)
+            if is_child(n - 3):
+                swap_h(n - 3)
+            if n < 2 * GRID1:
+                regroup_on_vector(n, VECTOR_UNITS[n][1:])
+            if is_child(n - 3):
+                group_h(n - 3)
+            if is_gchild(n - 2):
+                add_bias(n - 2 - GRID1)
+            if is_child(n - 3):
+                quantise_h(n - 3)
+            if is_gchild(n - 2):
+                finish(n - 2 - GRID1)

@@ -21,7 +21,7 @@ ROWS1 = 128
 ROWS2 = 32
 HI = C_MID // PACK
 
-VECTOR_UNITS = ((0, 2), (0, 2), (0, 1), (0, 1), (2,), (2, 3), (2,), (2, 3))
+VECTOR_UNITS = ((0, 2), (0, 2), (0, 1), (0, 1), (2, 3), (2, 3), (2,), (2, 3))
 
 FLOPS = 2 * 16 * ROWS1 * K * C_MID + 2 * 64 * ROWS2 * K * C_OUT
 
@@ -106,9 +106,9 @@ def tile_butterflylayer2d_pa_s_kernel(tc, x_parent, f_child, b_child, f_gchild, 
                 tiles.append(x_t)
             return tiles
 
-        def group_x(copy, bank, x_t):
+        def group_x(bank, x_t):
             x_grp_words = x_grp[:].bitcast(F32).rearrange("k (c f) -> k c f", f=8)
-            copy(out=x_grp_words[:, :, 4 * bank : 4 * bank + 4], in_=x_t[:].rearrange("k f c -> k c f"))
+            nc.scalar.copy(out=x_grp_words[:, :, 4 * bank : 4 * bank + 4], in_=x_t[:].rearrange("k f c -> k c f"))
 
         def transpose_biases():
             b_ps = psum_h.tile([P, GRID1 + 1, P], BF16, tag="h")
@@ -150,15 +150,17 @@ def tile_butterflylayer2d_pa_s_kernel(tc, x_parent, f_child, b_child, f_gchild, 
         def regroup_on_vector(c, units):
             regroup(nc.vector.tensor_copy, c, units)
 
-        def quantise_weights(c):
+        def quantise_weights(c, children=range(GRID1)):
             i = c % GRID1
+            nodes = slice(children.start, children.stop)
+            cols = slice(children.start * P, children.stop * P)
             if c < GRID1:
-                codes, scales, grouped = fc_codes, fc_scales, fc_grp[:, i].rearrange("k j c -> k (j c)")
+                codes, scales, grouped = fc_codes, fc_scales, fc_grp[:, i, nodes].rearrange("k j c -> k (j c)")
             else:
-                codes, scales, grouped = gc_codes, gc_scales, gc_grp[:, i].rearrange("k j a e c -> k (j a e c)")
-            nc.vector.quantize_mx(out=codes[:, i].bitcast(FP8X4), scales=scales[:, i], in_=grouped)
+                codes, scales, grouped = gc_codes, gc_scales, gc_grp[:, i, nodes].rearrange("k j a e c -> k (j a e c)")
+            nc.vector.quantize_mx(out=codes[:, i, cols].bitcast(FP8X4), scales=scales[:, i, cols], in_=grouped)
 
-        def multiply(c):
+        def multiply(c, children=range(GRID1)):
             i = c % GRID1
             if c < GRID1:
                 h_ps = psum_h.tile([P, GRID1 * ROWS1], F32, tag="h")
@@ -176,8 +178,11 @@ def tile_butterflylayer2d_pa_s_kernel(tc, x_parent, f_child, b_child, f_gchild, 
                     )
                 banks[c] = h_ps
             else:
-                o_ps = psum_o.tile([P, GRID1 * P], F32)
-                for j in range(GRID1):
+                if children.start == 0:
+                    o_tile = psum_o.tile([P, GRID1 * P], F32)
+                    banks[c] = o_tile
+                o_ps = banks[c]
+                for j in children:
                     cols = slice(j * P, (j + 1) * P)
                     nc.tensor.matmul_mx(
                         out=o_ps[:, cols],
@@ -188,7 +193,6 @@ def tile_butterflylayer2d_pa_s_kernel(tc, x_parent, f_child, b_child, f_gchild, 
                         start=True,
                         stop=True,
                     )
-                banks[c] = o_ps
 
         def activate_h(i):
             for j in range(GRID1):
@@ -237,11 +241,13 @@ def tile_butterflylayer2d_pa_s_kernel(tc, x_parent, f_child, b_child, f_gchild, 
 
         def finish(i):
             nc.scalar.activation(out=o_out[:, i].rearrange("k a e o -> k (a e o)"), in_=banks[GRID1 + i][:], func=RELU)
+
+        def store(pair):
             for j in range(GRID1):
-                for a in range(2):
+                for e in range(2):
                     nc.sync.dma_start(
-                        out=out[2 * i + a, 2 * j : 2 * j + 2].rearrange("e n y x o -> (n y x) e o"),
-                        in_=o_out[j * ROWS2 : (j + 1) * ROWS2, i, a],
+                        out=out[4 * pair : 4 * pair + 4, 2 * j + e].rearrange("g n y x o -> (n y x) g o"),
+                        in_=o_out[j * ROWS2 : (j + 1) * ROWS2, 2 * pair : 2 * pair + 2, :, e].rearrange("k i a o -> k (i a) o"),
                     )
 
         def is_child(c):
@@ -261,8 +267,8 @@ def tile_butterflylayer2d_pa_s_kernel(tc, x_parent, f_child, b_child, f_gchild, 
         quantise_weights(1)
         nc.vector.tensor_copy(out=bias[:], in_=b_ps[:, :, 0:16])
         regroup_on_vector(2, VECTOR_UNITS[2][:1])
-        group_x(nc.vector.tensor_copy, 0, x_banks[0])
-        group_x(nc.scalar.copy, 1, x_banks[1])
+        for bank in range(2):
+            group_x(bank, x_banks[bank])
         regroup_on_vector(2, VECTOR_UNITS[2][1:])
         nc.vector.quantize_mx(out=x_codes[:].bitcast(FP8X4), scales=x_scales[:], in_=x_grp[:])
         regroup_on_scalar(2)
@@ -270,26 +276,32 @@ def tile_butterflylayer2d_pa_s_kernel(tc, x_parent, f_child, b_child, f_gchild, 
         multiply(1)
         activate_h(0)
         transpose_h(0)
-        for n in range(3, 2 * GRID1 + 2):
+        last = 2 * GRID1 - 1
+        for n in range(3, last + 4):
             if is_child(n - 2):
                 activate_h(n - 2)
-            if n < 2 * GRID1:
+            if n <= last:
                 regroup_on_scalar(n)
                 regroup_on_vector(n, VECTOR_UNITS[n][:1])
-            if n <= 2 * GRID1:
-                quantise_weights(n - 1)
-                multiply(n - 1)
+            pieces = 2 if n - 1 == last else 1
+            if n - 1 <= last:
+                for piece in range(pieces):
+                    children = range(piece * GRID1 // pieces, (piece + 1) * GRID1 // pieces)
+                    quantise_weights(n - 1, children)
+                    multiply(n - 1, children)
             if is_child(n - 2):
                 transpose_h(n - 2)
             if is_child(n - 3):
                 swap_h(n - 3)
-            if n < 2 * GRID1:
+            if is_child(n - 4):
+                quantise_h(n - 4)
+            if n <= last:
                 regroup_on_vector(n, VECTOR_UNITS[n][1:])
             if is_child(n - 3):
                 group_h(n - 3)
             if is_gchild(n - 2):
                 add_bias(n - 2 - GRID1)
-            if is_child(n - 3):
-                quantise_h(n - 3)
-            if is_gchild(n - 2):
-                finish(n - 2 - GRID1)
+            if is_gchild(n - 3):
+                finish(n - 3 - GRID1)
+                if n % 2 == 0:
+                    store((n - 4 - GRID1) // 2)

@@ -8,7 +8,6 @@ BF16 = mybir.dt.bfloat16
 U32 = mybir.dt.uint32
 U8 = mybir.dt.uint8
 FP8X4 = mybir.dt.float8_e4m3fn_x4
-ADD = mybir.AluOpType.add
 RELU = mybir.ActivationFunctionType.Relu
 
 P = 128
@@ -20,6 +19,9 @@ C_OUT = 32
 ROWS1 = 128
 ROWS2 = 32
 HI = C_MID // PACK
+
+ROW = range(GRID1)
+HALVES = (range(2), range(2, GRID1))
 
 VECTOR_UNITS = ((0, 2), (0, 2), (0, 1), (0, 1), (2, 3), (2, 3), (2,), (2, 3))
 
@@ -34,7 +36,6 @@ def tile_butterflylayer2d_pa_s_kernel(tc, x_parent, f_child, b_child, f_gchild, 
         psum_early = ctx.enter_context(tc.psum_pool(name="psum_early", bufs=2))
         psum_h = ctx.enter_context(tc.psum_pool(name="psum_h", bufs=2))
         psum_o = ctx.enter_context(tc.psum_pool(name="psum_o", bufs=2))
-        psum_t = ctx.enter_context(tc.psum_pool(name="psum_t", bufs=2))
         ctx.enter_context(tc.manual_schedule())
 
         fc_raw = keep.tile([P, GRID1, GRID1, PACK * C_MID], BF16)
@@ -48,8 +49,9 @@ def tile_butterflylayer2d_pa_s_kernel(tc, x_parent, f_child, b_child, f_gchild, 
                 )
 
         def load_gchild(i):
-            for a in range(2):
-                for half in range(2):
+            for first in range(2):
+                for second in range(2):
+                    half, a = (first, second) if i == GRID1 - 1 else (second, first)
                     nodes = slice(4 * half, 4 * half + 4)
                     nc.sync.dma_start(
                         out=gc_raw[:, i, a, nodes],
@@ -126,10 +128,10 @@ def tile_butterflylayer2d_pa_s_kernel(tc, x_parent, f_child, b_child, f_gchild, 
         h_grp = keep.tile([P, GRID1, GRID1 * ROWS2 * PACK], BF16, align_bytes=64)
         h_codes = keep.tile([P, GRID1, GRID1 * ROWS2], U32, align_bytes=64)
         h_scales = keep.tile([P, GRID1, GRID1 * ROWS2], U8, align_bytes=64)
-        o_out = keep.tile([P, GRID1, 2, 2, C_OUT], F32)
+        o_out = keep.tile([P, GRID1, GRID1 * C_OUT], F32, align_bytes=64)
         banks = {}
 
-        def regroup(copy, c, units):
+        def regroup(copy, c, units, children):
             i = c % GRID1
             for unit in units:
                 if c < GRID1:
@@ -140,17 +142,17 @@ def tile_butterflylayer2d_pa_s_kernel(tc, x_parent, f_child, b_child, f_gchild, 
                 else:
                     a, e = divmod(unit, 2)
                     copy(
-                        out=gc_grp[:, i, :, a, e].rearrange("k j (h m r) -> k j h r m", m=4, r=PACK),
-                        in_=gc_raw[:, i, a, e : 8 : 2].rearrange("k j (r h m) -> k j h r m", r=PACK, m=4),
+                        out=gc_grp[:, i, children.start : children.stop, a, e].rearrange("k j (h m r) -> k j h r m", m=4, r=PACK),
+                        in_=gc_raw[:, i, a, 2 * children.start + e : 2 * children.stop : 2].rearrange("k j (r h m) -> k j h r m", r=PACK, m=4),
                     )
 
-        def regroup_on_scalar(c):
-            regroup(nc.scalar.copy, c, [unit for unit in range(4) if unit not in VECTOR_UNITS[c]])
+        def regroup_on_scalar(c, children=ROW):
+            regroup(nc.scalar.copy, c, [unit for unit in range(4) if unit not in VECTOR_UNITS[c]], children)
 
-        def regroup_on_vector(c, units):
-            regroup(nc.vector.tensor_copy, c, units)
+        def regroup_on_vector(c, units, children=ROW):
+            regroup(nc.vector.tensor_copy, c, units, children)
 
-        def quantise_weights(c, children=range(GRID1)):
+        def quantise_weights(c, children=ROW):
             i = c % GRID1
             nodes = slice(children.start, children.stop)
             cols = slice(children.start * P, children.stop * P)
@@ -160,7 +162,7 @@ def tile_butterflylayer2d_pa_s_kernel(tc, x_parent, f_child, b_child, f_gchild, 
                 codes, scales, grouped = gc_codes, gc_scales, gc_grp[:, i, nodes].rearrange("k j a e c -> k (j a e c)")
             nc.vector.quantize_mx(out=codes[:, i, cols].bitcast(FP8X4), scales=scales[:, i, cols], in_=grouped)
 
-        def multiply(c, children=range(GRID1)):
+        def multiply(c, children=ROW):
             i = c % GRID1
             if c < GRID1:
                 h_ps = psum_h.tile([P, GRID1 * ROWS1], F32, tag="h")
@@ -224,31 +226,28 @@ def tile_butterflylayer2d_pa_s_kernel(tc, x_parent, f_child, b_child, f_gchild, 
                 in_=banks[i][:].rearrange("k (j v w) -> k j w v", j=GRID1, v=2),
             )
 
-        def add_bias(i):
-            o_sum = work.tile([P, GRID1, ROWS2], F32)
-            nc.vector.tensor_tensor(
-                out=o_sum[:],
-                in0=banks[GRID1 + i][:].rearrange("m (x w) -> m x w", w=ROWS2)[:, 0 : GRID1 * GRID1 : GRID1 + 1, :],
-                in1=bias[:, i, 0:GRID1].unsqueeze(2).to_broadcast([P, GRID1, ROWS2]),
-                op=ADD,
-            )
-            o_t = psum_t.tile([P, P], F32)
-            nc.tensor.transpose(o_t[:], o_sum[:].rearrange("m j w -> m (j w)"), ident[:])
-            banks[GRID1 + i] = o_t
+        def activate_o(i):
+            o_act = work.tile([P, GRID1 * ROWS2], F32, align_bytes=64)
+            for j in range(GRID1):
+                wanted = slice(j * P + j * ROWS2, j * P + (j + 1) * ROWS2)
+                nc.scalar.activation(
+                    out=o_act[:, j * ROWS2 : (j + 1) * ROWS2],
+                    in_=banks[GRID1 + i][:, wanted],
+                    func=RELU,
+                    bias=bias[:, i, j : j + 1],
+                )
+            banks[GRID1 + i] = o_act
+
+        def turn_and_store(i):
+            nc.vector.transpose(out=o_out[:, i], in_=banks[GRID1 + i][:])
+            for a in range(2):
+                nc.sync.dma_start(
+                    out=out[2 * i + a].rearrange("(j e) n y x o -> (e n y x) j o", e=2),
+                    in_=o_out[a * 2 * ROWS2 : (a + 1) * 2 * ROWS2, i].rearrange("k (j o) -> k j o", j=GRID1),
+                )
 
         def quantise_h(c):
             nc.vector.quantize_mx(out=h_codes[:, c].bitcast(FP8X4), scales=h_scales[:, c], in_=h_grp[:, c])
-
-        def finish(i):
-            nc.scalar.activation(out=o_out[:, i].rearrange("k a e o -> k (a e o)"), in_=banks[GRID1 + i][:], func=RELU)
-
-        def store(pair):
-            for j in range(GRID1):
-                for e in range(2):
-                    nc.sync.dma_start(
-                        out=out[4 * pair : 4 * pair + 4, 2 * j + e].rearrange("g n y x o -> (n y x) g o"),
-                        in_=o_out[j * ROWS2 : (j + 1) * ROWS2, 2 * pair : 2 * pair + 2, :, e].rearrange("k i a o -> k (i a) o"),
-                    )
 
         def is_child(c):
             return 0 <= c < GRID1
@@ -280,28 +279,33 @@ def tile_butterflylayer2d_pa_s_kernel(tc, x_parent, f_child, b_child, f_gchild, 
         for n in range(3, last + 4):
             if is_child(n - 2):
                 activate_h(n - 2)
-            if n <= last:
+            if n < last:
                 regroup_on_scalar(n)
                 regroup_on_vector(n, VECTOR_UNITS[n][:1])
-            pieces = 2 if n - 1 == last else 1
-            if n - 1 <= last:
-                for piece in range(pieces):
-                    children = range(piece * GRID1 // pieces, (piece + 1) * GRID1 // pieces)
-                    quantise_weights(n - 1, children)
-                    multiply(n - 1, children)
+            elif n == last:
+                for children in HALVES:
+                    regroup_on_scalar(n, children)
+                regroup_on_vector(n, VECTOR_UNITS[n], HALVES[0])
+            if n - 1 < last:
+                quantise_weights(n - 1)
+                multiply(n - 1)
+            elif n - 1 == last:
+                quantise_weights(last, HALVES[0])
+                multiply(last, HALVES[0])
+                regroup_on_vector(last, VECTOR_UNITS[last], HALVES[1])
+                quantise_weights(last, HALVES[1])
+                multiply(last, HALVES[1])
             if is_child(n - 2):
                 transpose_h(n - 2)
             if is_child(n - 3):
                 swap_h(n - 3)
             if is_child(n - 4):
                 quantise_h(n - 4)
-            if n <= last:
+            if n < last:
                 regroup_on_vector(n, VECTOR_UNITS[n][1:])
             if is_child(n - 3):
                 group_h(n - 3)
-            if is_gchild(n - 2):
-                add_bias(n - 2 - GRID1)
             if is_gchild(n - 3):
-                finish(n - 3 - GRID1)
-                if n % 2 == 0:
-                    store((n - 4 - GRID1) // 2)
+                turn_and_store(n - 3 - GRID1)
+            if is_gchild(n - 2):
+                activate_o(n - 2 - GRID1)

@@ -23,7 +23,7 @@ HI = C_MID // PACK
 ROW = range(GRID1)
 HALVES = (range(2), range(2, GRID1))
 
-VECTOR_UNITS = ((0, 2), (0, 2), (0, 1), (0, 1), (2, 3), (2, 3), (2,), (2, 3))
+VECTOR_UNITS = ((2, 3), (2, 3), (2, 3), (2, 3), (2, 3), (2, 3), (2,), (2, 3))
 
 FLOPS = 2 * 16 * ROWS1 * K * C_MID + 2 * 64 * ROWS2 * K * C_OUT
 
@@ -41,11 +41,11 @@ def tile_butterflylayer2d_pa_s_kernel(tc, x_parent, f_child, b_child, f_gchild, 
         fc_raw = keep.tile([P, GRID1, GRID1, PACK * C_MID], BF16)
         gc_raw = keep.tile([P, GRID1, 2, 8, PACK * C_OUT], BF16)
 
-        def load_child(i, width):
-            for j in range(0, GRID1, width):
+        def load_child(i):
+            for nodes in (slice(0, 2), slice(2, 4)):
                 nc.sync.dma_start(
-                    out=fc_raw[:, i, j : j + width],
-                    in_=f_child[i, j : j + width].rearrange("j p q (h l) o -> (p q h) j (l o)", l=PACK),
+                    out=fc_raw[:, i, nodes],
+                    in_=f_child[i, nodes].rearrange("j p q (h l) o -> (p q h) j (l o)", l=PACK),
                 )
 
         def load_gchild(i):
@@ -58,8 +58,11 @@ def tile_butterflylayer2d_pa_s_kernel(tc, x_parent, f_child, b_child, f_gchild, 
                         in_=f_gchild[2 * i + a, nodes].rearrange("j p q (h l) o -> (p q h) j (l o)", l=PACK),
                     )
 
-        load_child(0, 1)
-        load_child(1, 2)
+        x_rows = keep.tile([P, 4, K], BF16)
+        patches = x_parent.rearrange("u v n (y p) (s d q) c -> d p (u v n y) s (q c)", p=2, s=4, d=2)
+        for d in range(2):
+            for p in range(2):
+                nc.sync.dma_start(out=x_rows[d:P:2, :, p * 256 : (p + 1) * 256], in_=patches[d, p])
         b_rows = keep.tile([P, GRID1 + 1, P], BF16)
         nc.vector.memset(b_rows[:], 0.0)
         nc.sync.dma_start(out=b_rows[0:16, GRID1, :], in_=b_child.rearrange("i j c -> (i j) c"))
@@ -67,13 +70,8 @@ def tile_butterflylayer2d_pa_s_kernel(tc, x_parent, f_child, b_child, f_gchild, 
             out=b_rows[0:GRID1, 0:GRID1, :].rearrange("j i (a f) -> j (i a) f", a=2),
             in_=b_gchild.rearrange("i (j e) o -> j i (e o)", e=2),
         )
-        x_rows = keep.tile([P, 4, K], BF16)
-        patches = x_parent.rearrange("u v n (y p) (s d q) c -> d p (u v n y) s (q c)", p=2, s=4, d=2)
-        for d in range(2):
-            for p in range(2):
-                nc.sync.dma_start(out=x_rows[d:P:2, :, p * 256 : (p + 1) * 256], in_=patches[d, p])
-        for i in range(2, GRID1):
-            load_child(i, 2)
+        for i in range(GRID1):
+            load_child(i)
         for i in range(GRID1):
             load_gchild(i)
 
@@ -108,9 +106,9 @@ def tile_butterflylayer2d_pa_s_kernel(tc, x_parent, f_child, b_child, f_gchild, 
                 tiles.append(x_t)
             return tiles
 
-        def group_x(bank, x_t):
+        def group_x(copy, bank, x_t):
             x_grp_words = x_grp[:].bitcast(F32).rearrange("k (c f) -> k c f", f=8)
-            nc.scalar.copy(out=x_grp_words[:, :, 4 * bank : 4 * bank + 4], in_=x_t[:].rearrange("k f c -> k c f"))
+            copy(out=x_grp_words[:, :, 4 * bank : 4 * bank + 4], in_=x_t[:].rearrange("k f c -> k c f"))
 
         def transpose_biases():
             b_ps = psum_h.tile([P, GRID1 + 1, P], BF16, tag="h")
@@ -133,13 +131,14 @@ def tile_butterflylayer2d_pa_s_kernel(tc, x_parent, f_child, b_child, f_gchild, 
 
         def regroup(copy, c, units, children):
             i = c % GRID1
-            for unit in units:
-                if c < GRID1:
-                    copy(
-                        out=fc_grp[:, i, unit].rearrange("k (h m r) -> k h r m", m=4, r=PACK),
-                        in_=fc_raw[:, i, unit].rearrange("k (r h m) -> k h r m", r=PACK, m=4),
-                    )
-                else:
+            if c < GRID1:
+                nodes = slice(units[0], units[-1] + 1)
+                copy(
+                    out=fc_grp[:, i, nodes].rearrange("k j (h m r) -> k j h r m", m=4, r=PACK),
+                    in_=fc_raw[:, i, nodes].rearrange("k j (r h m) -> k j h r m", r=PACK, m=4),
+                )
+            else:
+                for unit in units:
                     a, e = divmod(unit, 2)
                     copy(
                         out=gc_grp[:, i, children.start : children.stop, a, e].rearrange("k j (h m r) -> k j h r m", m=4, r=PACK),
@@ -255,38 +254,24 @@ def tile_butterflylayer2d_pa_s_kernel(tc, x_parent, f_child, b_child, f_gchild, 
         def is_gchild(c):
             return GRID1 <= c < 2 * GRID1
 
-        regroup_on_scalar(0)
-        regroup_on_vector(0, VECTOR_UNITS[0])
-        regroup_on_scalar(1)
-        regroup_on_vector(1, VECTOR_UNITS[1][:1])
-        quantise_weights(0)
-        regroup_on_vector(1, VECTOR_UNITS[1][1:])
-        b_ps = transpose_biases()
         x_banks = transpose_x()
-        quantise_weights(1)
-        nc.vector.tensor_copy(out=bias[:], in_=b_ps[:, :, 0:16])
-        regroup_on_vector(2, VECTOR_UNITS[2][:1])
-        for bank in range(2):
-            group_x(bank, x_banks[bank])
-        regroup_on_vector(2, VECTOR_UNITS[2][1:])
-        nc.vector.quantize_mx(out=x_codes[:].bitcast(FP8X4), scales=x_scales[:], in_=x_grp[:])
-        regroup_on_scalar(2)
-        multiply(0)
-        multiply(1)
-        activate_h(0)
-        transpose_h(0)
+        b_ps = transpose_biases()
         last = 2 * GRID1 - 1
-        for n in range(3, last + 4):
-            if is_child(n - 2):
-                activate_h(n - 2)
+        for n in range(last + 4):
             if n < last:
                 regroup_on_scalar(n)
-                regroup_on_vector(n, VECTOR_UNITS[n][:1])
             elif n == last:
                 for children in HALVES:
                     regroup_on_scalar(n, children)
-                regroup_on_vector(n, VECTOR_UNITS[n], HALVES[0])
-            if n - 1 < last:
+            if is_child(n - 2):
+                activate_h(n - 2)
+            if n == 0:
+                group_x(nc.vector.tensor_copy, 0, x_banks[0])
+                group_x(nc.scalar.copy, 1, x_banks[1])
+                nc.vector.tensor_copy(out=bias[:], in_=b_ps[:, :, 0:16])
+            if n == 1:
+                nc.vector.quantize_mx(out=x_codes[:].bitcast(FP8X4), scales=x_scales[:], in_=x_grp[:])
+            if 0 <= n - 1 < last:
                 quantise_weights(n - 1)
                 multiply(n - 1)
             elif n - 1 == last:
@@ -297,11 +282,17 @@ def tile_butterflylayer2d_pa_s_kernel(tc, x_parent, f_child, b_child, f_gchild, 
                 multiply(last, HALVES[1])
             if is_child(n - 2):
                 transpose_h(n - 2)
+            if is_child(n):
+                regroup_on_vector(n, VECTOR_UNITS[n])
+            elif n < last:
+                regroup_on_vector(n, VECTOR_UNITS[n][:1])
+            elif n == last:
+                regroup_on_vector(n, VECTOR_UNITS[n], HALVES[0])
             if is_child(n - 3):
                 swap_h(n - 3)
             if is_child(n - 4):
                 quantise_h(n - 4)
-            if n < last:
+            if GRID1 <= n < last:
                 regroup_on_vector(n, VECTOR_UNITS[n][1:])
             if is_child(n - 3):
                 group_h(n - 3)

@@ -23,7 +23,7 @@ HI = C_MID // PACK
 ROW = range(GRID1)
 HALVES = (range(2), range(2, GRID1))
 
-VECTOR_UNITS = ((2, 3), (2, 3), (2, 3), (2, 3), (2, 3), (2, 3), (2,), (2, 3))
+VECTOR_UNITS = ((2, 3), (2, 3), (1, 2, 3), (1, 2, 3), (2, 3), (2, 3), (2, 3), (2, 3))
 
 FLOPS = 2 * 16 * ROWS1 * K * C_MID + 2 * 64 * ROWS2 * K * C_OUT
 
@@ -63,6 +63,7 @@ def tile_butterflylayer2d_pa_s_kernel(tc, x_parent, f_child, b_child, f_gchild, 
         for d in range(2):
             for p in range(2):
                 nc.sync.dma_start(out=x_rows[d:P:2, :, p * 256 : (p + 1) * 256], in_=patches[d, p])
+        load_child(0)
         b_rows = keep.tile([P, GRID1 + 1, P], BF16)
         nc.vector.memset(b_rows[:], 0.0)
         nc.sync.dma_start(out=b_rows[0:16, GRID1, :], in_=b_child.rearrange("i j c -> (i j) c"))
@@ -70,7 +71,7 @@ def tile_butterflylayer2d_pa_s_kernel(tc, x_parent, f_child, b_child, f_gchild, 
             out=b_rows[0:GRID1, 0:GRID1, :].rearrange("j i (a f) -> j (i a) f", a=2),
             in_=b_gchild.rearrange("i (j e) o -> j i (e o)", e=2),
         )
-        for i in range(GRID1):
+        for i in range(1, GRID1):
             load_child(i)
         for i in range(GRID1):
             load_gchild(i)

@@ -18,12 +18,12 @@ C_MID = 128
 C_OUT = 32
 ROWS1 = 128
 ROWS2 = 32
-HI = C_MID // PACK
+RUN = 8
 
 ROW = range(GRID1)
 HALVES = (range(2), range(2, GRID1))
 
-VECTOR_UNITS = ((2, 3), (2, 3), (1, 2, 3), (1, 2, 3), (2, 3), (2, 3), (2, 3), (2, 3))
+VECTOR_UNITS = ((2, 3), (2, 3), (2, 3), (2, 3), (2, 3), (2,), (2,), (2,))
 
 FLOPS = 2 * 16 * ROWS1 * K * C_MID + 2 * 64 * ROWS2 * K * C_OUT
 
@@ -135,15 +135,15 @@ def tile_butterflylayer2d_pa_s_kernel(tc, x_parent, f_child, b_child, f_gchild, 
             if c < GRID1:
                 nodes = slice(units[0], units[-1] + 1)
                 copy(
-                    out=fc_grp[:, i, nodes].rearrange("k j (h m r) -> k j h r m", m=4, r=PACK),
-                    in_=fc_raw[:, i, nodes].rearrange("k j (r h m) -> k j h r m", r=PACK, m=4),
+                    out=fc_grp[:, i, nodes].rearrange("k j (h m r) -> k j h r m", m=RUN, r=PACK),
+                    in_=fc_raw[:, i, nodes].rearrange("k j (r h m) -> k j h r m", r=PACK, m=RUN),
                 )
             else:
                 for unit in units:
                     a, e = divmod(unit, 2)
                     copy(
-                        out=gc_grp[:, i, children.start : children.stop, a, e].rearrange("k j (h m r) -> k j h r m", m=4, r=PACK),
-                        in_=gc_raw[:, i, a, 2 * children.start + e : 2 * children.stop : 2].rearrange("k j (r h m) -> k j h r m", r=PACK, m=4),
+                        out=gc_grp[:, i, children.start : children.stop, a, e].rearrange("k j (h m r) -> k j h r m", m=RUN, r=PACK),
+                        in_=gc_raw[:, i, a, 2 * children.start + e : 2 * children.stop : 2].rearrange("k j (r h m) -> k j h r m", r=PACK, m=RUN),
                     )
 
         def regroup_on_scalar(c, children=ROW):
@@ -269,7 +269,6 @@ def tile_butterflylayer2d_pa_s_kernel(tc, x_parent, f_child, b_child, f_gchild, 
             if n == 0:
                 group_x(nc.vector.tensor_copy, 0, x_banks[0])
                 group_x(nc.scalar.copy, 1, x_banks[1])
-                nc.vector.tensor_copy(out=bias[:], in_=b_ps[:, :, 0:16])
             if n == 1:
                 nc.vector.quantize_mx(out=x_codes[:].bitcast(FP8X4), scales=x_scales[:], in_=x_grp[:])
             if 0 <= n - 1 < last:
@@ -285,6 +284,8 @@ def tile_butterflylayer2d_pa_s_kernel(tc, x_parent, f_child, b_child, f_gchild, 
                 transpose_h(n - 2)
             if is_child(n):
                 regroup_on_vector(n, VECTOR_UNITS[n])
+                if n == 1:
+                    nc.vector.tensor_copy(out=bias[:], in_=b_ps[:, :, 0:16])
             elif n < last:
                 regroup_on_vector(n, VECTOR_UNITS[n][:1])
             elif n == last:

@@ -42,7 +42,9 @@ def tile_butterflylayer2d_pa_s_kernel(tc, x_parent, f_child, b_child, f_gchild, 
         gc_raw = keep.tile([P, GRID1, 2, 8, PACK * C_OUT], BF16)
 
         def load_child(i):
-            for nodes in (slice(0, 2), slice(2, 4)):
+            width = 1 if i == 0 else 2
+            for j in range(0, GRID1, width):
+                nodes = slice(j, j + width)
                 nc.sync.dma_start(
                     out=fc_raw[:, i, nodes],
                     in_=f_child[i, nodes].rearrange("j p q (h l) o -> (p q h) j (l o)", l=PACK),
@@ -133,11 +135,13 @@ def tile_butterflylayer2d_pa_s_kernel(tc, x_parent, f_child, b_child, f_gchild, 
         def regroup(copy, c, units, children):
             i = c % GRID1
             if c < GRID1:
-                nodes = slice(units[0], units[-1] + 1)
-                copy(
-                    out=fc_grp[:, i, nodes].rearrange("k j (h m r) -> k j h r m", m=RUN, r=PACK),
-                    in_=fc_raw[:, i, nodes].rearrange("k j (r h m) -> k j h r m", r=PACK, m=RUN),
-                )
+                width = 1 if c == 0 else len(units)
+                for first in range(units[0], units[-1] + 1, width):
+                    nodes = slice(first, first + width)
+                    copy(
+                        out=fc_grp[:, i, nodes].rearrange("k j (h m r) -> k j h r m", m=RUN, r=PACK),
+                        in_=fc_raw[:, i, nodes].rearrange("k j (r h m) -> k j h r m", r=PACK, m=RUN),
+                    )
             else:
                 for unit in units:
                     a, e = divmod(unit, 2)
@@ -262,8 +266,9 @@ def tile_butterflylayer2d_pa_s_kernel(tc, x_parent, f_child, b_child, f_gchild, 
             if n < last:
                 regroup_on_scalar(n)
             elif n == last:
-                for children in HALVES:
-                    regroup_on_scalar(n, children)
+                regroup_on_scalar(n, HALVES[0])
+                activate_o(n - 2 - GRID1)
+                regroup_on_scalar(n, HALVES[1])
             if is_child(n - 2):
                 activate_h(n - 2)
             if n == 0:
@@ -300,5 +305,5 @@ def tile_butterflylayer2d_pa_s_kernel(tc, x_parent, f_child, b_child, f_gchild, 
                 group_h(n - 3)
             if is_gchild(n - 3):
                 turn_and_store(n - 3 - GRID1)
-            if is_gchild(n - 2):
+            if is_gchild(n - 2) and n != last:
                 activate_o(n - 2 - GRID1)

@@ -23,7 +23,7 @@ RUN = 8
 ROW = range(GRID1)
 HALVES = (range(2), range(2, GRID1))
 
-VECTOR_UNITS = ((2, 3), (2, 3), (2, 3), (2, 3), (2, 3), (2,), (2,), (2,))
+VECTOR_UNITS = ((3,), (2, 3), (2, 3), (2, 3), (2, 3), (2,), (2,), (2,))
 
 FLOPS = 2 * 16 * ROWS1 * K * C_MID + 2 * 64 * ROWS2 * K * C_OUT
 
@@ -263,7 +263,12 @@ def tile_butterflylayer2d_pa_s_kernel(tc, x_parent, f_child, b_child, f_gchild, 
         b_ps = transpose_biases()
         last = 2 * GRID1 - 1
         for n in range(last + 4):
-            if n < last:
+            if n == 0:
+                regroup(nc.scalar.copy, 0, (0, 1), ROW)
+                group_x(nc.vector.tensor_copy, 0, x_banks[0])
+                group_x(nc.scalar.copy, 1, x_banks[1])
+                regroup(nc.scalar.copy, 0, (2,), ROW)
+            elif n < last:
                 regroup_on_scalar(n)
             elif n == last:
                 regroup_on_scalar(n, HALVES[0])
@@ -271,9 +276,6 @@ def tile_butterflylayer2d_pa_s_kernel(tc, x_parent, f_child, b_child, f_gchild, 
                 regroup_on_scalar(n, HALVES[1])
             if is_child(n - 2):
                 activate_h(n - 2)
-            if n == 0:
-                group_x(nc.vector.tensor_copy, 0, x_banks[0])
-                group_x(nc.scalar.copy, 1, x_banks[1])
             if n == 1:
                 nc.vector.quantize_mx(out=x_codes[:].bitcast(FP8X4), scales=x_scales[:], in_=x_grp[:])
             if 0 <= n - 1 < last:

from contextlib import ExitStack

import concourse.mybir as mybir
from concourse.masks import make_identity

F32 = mybir.dt.float32
BF16 = mybir.dt.bfloat16
U32 = mybir.dt.uint32
U8 = mybir.dt.uint8
FP8X4 = mybir.dt.float8_e4m3fn_x4
RELU = mybir.ActivationFunctionType.Relu

P = 128
PACK = 4
K = P * PACK
GRID1 = 4
C_MID = 128
C_OUT = 32
ROWS1 = 128
ROWS2 = 32
RUN = 8

ROW = range(GRID1)
HALVES = (range(2), range(2, GRID1))

VECTOR_UNITS = ((3,), (2, 3), (2, 3), (2, 3), (2, 3), (2,), (2,), (2,))

FLOPS = 2 * 16 * ROWS1 * K * C_MID + 2 * 64 * ROWS2 * K * C_OUT


def tile_butterflylayer2d_pa_s_kernel(tc, x_parent, f_child, b_child, f_gchild, b_gchild, out):
    nc = tc.nc
    with ExitStack() as ctx:
        keep = ctx.enter_context(tc.tile_pool(name="keep", bufs=1))
        work = ctx.enter_context(tc.tile_pool(name="work", bufs=2))
        psum_early = ctx.enter_context(tc.psum_pool(name="psum_early", bufs=2))
        psum_h = ctx.enter_context(tc.psum_pool(name="psum_h", bufs=2))
        psum_o = ctx.enter_context(tc.psum_pool(name="psum_o", bufs=2))
        ctx.enter_context(tc.manual_schedule())

        fc_raw = keep.tile([P, GRID1, GRID1, PACK * C_MID], BF16)
        gc_raw = keep.tile([P, GRID1, 2, 8, PACK * C_OUT], BF16)

        def load_child(i):
            width = 1 if i == 0 else 2
            for j in range(0, GRID1, width):
                nodes = slice(j, j + width)
                nc.sync.dma_start(
                    out=fc_raw[:, i, nodes],
                    in_=f_child[i, nodes].rearrange("j p q (h l) o -> (p q h) j (l o)", l=PACK),
                )

        def load_gchild(i):
            for first in range(2):
                for second in range(2):
                    half, a = (first, second) if i == GRID1 - 1 else (second, first)
                    nodes = slice(4 * half, 4 * half + 4)
                    nc.sync.dma_start(
                        out=gc_raw[:, i, a, nodes],
                        in_=f_gchild[2 * i + a, nodes].rearrange("j p q (h l) o -> (p q h) j (l o)", l=PACK),
                    )

        x_rows = keep.tile([P, 4, K], BF16)
        patches = x_parent.rearrange("u v n (y p) (s d q) c -> d p (u v n y) s (q c)", p=2, s=4, d=2)
        for d in range(2):
            for p in range(2):
                nc.sync.dma_start(out=x_rows[d:P:2, :, p * 256 : (p + 1) * 256], in_=patches[d, p])
        load_child(0)
        b_rows = keep.tile([P, GRID1 + 1, P], BF16)
        nc.vector.memset(b_rows[:], 0.0)
        nc.sync.dma_start(out=b_rows[0:16, GRID1, :], in_=b_child.rearrange("i j c -> (i j) c"))
        nc.sync.dma_start(
            out=b_rows[0:GRID1, 0:GRID1, :].rearrange("j i (a f) -> j (i a) f", a=2),
            in_=b_gchild.rearrange("i (j e) o -> j i (e o)", e=2),
        )
        for i in range(1, GRID1):
            load_child(i)
        for i in range(GRID1):
            load_gchild(i)

        ident = keep.tile([P, P], F32)
        make_identity(nc, ident[:])
        ident_bf = keep.tile([P, P], BF16)
        nc.vector.tensor_copy(out=ident_bf[:], in_=ident[:])
        sort_channels = keep.tile([P, P], BF16)
        nc.vector.tensor_copy(
            out=sort_channels[:].rearrange("c (v h s) -> c v h s", v=2, s=2),
            in_=ident[:].rearrange("c (h v s) -> c v h s", v=2, s=2),
        )
        sort_pixels = keep.tile([P, P], F32)
        nc.vector.tensor_copy(
            out=sort_pixels[:].rearrange("r (g t a) -> r g t a", g=4, t=4),
            in_=ident[:].rearrange("r (g a t) -> r g t a", g=4, t=4),
        )

        x_grp = keep.tile([P, 4 * ROWS1 * PACK], BF16, align_bytes=64)
        x_codes = keep.tile([P, 4 * ROWS1], U32, align_bytes=64)
        x_scales = keep.tile([P, 4 * ROWS1], U8, align_bytes=64)
        bias = keep.tile([P, GRID1 + 1, 16], F32)

        def transpose_x():
            x_words = x_rows[:].bitcast(F32).rearrange("c s (k v) -> c s k v", v=2)
            tiles = []
            for bank in range(2):
                x_t = psum_early.tile([P, 4, P], F32, tag="early")
                for s in range(2):
                    for v in range(2):
                        nc.tensor.transpose(x_t[:, 2 * s + v, :], x_words[:, 2 * bank + s, :, v], sort_pixels[:])
                tiles.append(x_t)
            return tiles

        def group_x(copy, bank, x_t):
            x_grp_words = x_grp[:].bitcast(F32).rearrange("k (c f) -> k c f", f=8)
            copy(out=x_grp_words[:, :, 4 * bank : 4 * bank + 4], in_=x_t[:].rearrange("k f c -> k c f"))

        def transpose_biases():
            b_ps = psum_h.tile([P, GRID1 + 1, P], BF16, tag="h")
            for i in range(GRID1 + 1):
                nc.tensor.transpose(b_ps[:, i, :], b_rows[:, i, :], ident_bf[:])
            return b_ps

        fc_grp = keep.tile([P, GRID1, GRID1, C_MID * PACK], BF16, align_bytes=64)
        fc_codes = keep.tile([P, GRID1, GRID1 * C_MID], U32, align_bytes=64)
        fc_scales = keep.tile([P, GRID1, GRID1 * C_MID], U8, align_bytes=64)
        gc_grp = keep.tile([P, GRID1, GRID1, 2, 2, C_OUT * PACK], BF16, align_bytes=64)
        gc_codes = keep.tile([P, GRID1, GRID1 * P], U32, align_bytes=64)
        gc_scales = keep.tile([P, GRID1, GRID1 * P], U8, align_bytes=64)
        h_rows = keep.tile([P, GRID1, GRID1, ROWS1], BF16)
        h_grp = keep.tile([P, GRID1, GRID1 * ROWS2 * PACK], BF16, align_bytes=64)
        h_codes = keep.tile([P, GRID1, GRID1 * ROWS2], U32, align_bytes=64)
        h_scales = keep.tile([P, GRID1, GRID1 * ROWS2], U8, align_bytes=64)
        o_out = keep.tile([P, GRID1, GRID1 * C_OUT], F32, align_bytes=64)
        banks = {}

        def regroup(copy, c, units, children):
            i = c % GRID1
            if c < GRID1:
                width = 1 if c == 0 else len(units)
                for first in range(units[0], units[-1] + 1, width):
                    nodes = slice(first, first + width)
                    copy(
                        out=fc_grp[:, i, nodes].rearrange("k j (h m r) -> k j h r m", m=RUN, r=PACK),
                        in_=fc_raw[:, i, nodes].rearrange("k j (r h m) -> k j h r m", r=PACK, m=RUN),
                    )
            else:
                for unit in units:
                    a, e = divmod(unit, 2)
                    copy(
                        out=gc_grp[:, i, children.start : children.stop, a, e].rearrange("k j (h m r) -> k j h r m", m=RUN, r=PACK),
                        in_=gc_raw[:, i, a, 2 * children.start + e : 2 * children.stop : 2].rearrange("k j (r h m) -> k j h r m", r=PACK, m=RUN),
                    )

        def regroup_on_scalar(c, children=ROW):
            regroup(nc.scalar.copy, c, [unit for unit in range(4) if unit not in VECTOR_UNITS[c]], children)

        def regroup_on_vector(c, units, children=ROW):
            regroup(nc.vector.tensor_copy, c, units, children)

        def quantise_weights(c, children=ROW):
            i = c % GRID1
            nodes = slice(children.start, children.stop)
            cols = slice(children.start * P, children.stop * P)
            if c < GRID1:
                codes, scales, grouped = fc_codes, fc_scales, fc_grp[:, i, nodes].rearrange("k j c -> k (j c)")
            else:
                codes, scales, grouped = gc_codes, gc_scales, gc_grp[:, i, nodes].rearrange("k j a e c -> k (j a e c)")
            nc.vector.quantize_mx(out=codes[:, i, cols].bitcast(FP8X4), scales=scales[:, i, cols], in_=grouped)

        def multiply(c, children=ROW):
            i = c % GRID1
            if c < GRID1:
                h_ps = psum_h.tile([P, GRID1 * ROWS1], F32, tag="h")
                for j in range(GRID1):
                    g = 2 * (i // 2) + j // 2
                    cols = slice(j * C_MID, (j + 1) * C_MID)
                    nc.tensor.matmul_mx(
                        out=h_ps[:, j * ROWS1 : (j + 1) * ROWS1],
                        lhsT=fc_codes[:, i, cols].bitcast(FP8X4),
                        lhsT_scale=fc_scales[:, i, cols],
                        rhs=x_codes[:, g * ROWS1 : (g + 1) * ROWS1].bitcast(FP8X4),
                        rhs_scale=x_scales[:, g * ROWS1 : (g + 1) * ROWS1],
                        start=True,
                        stop=True,
                    )
                banks[c] = h_ps
            else:
                if children.start == 0:
                    o_tile = psum_o.tile([P, GRID1 * P], F32)
                    banks[c] = o_tile
                o_ps = banks[c]
                for j in children:
                    cols = slice(j * P, (j + 1) * P)
                    nc.tensor.matmul_mx(
                        out=o_ps[:, cols],
                        lhsT=gc_codes[:, i, cols].bitcast(FP8X4),
                        lhsT_scale=gc_scales[:, i, cols],
                        rhs=h_codes[:, i].bitcast(FP8X4),
                        rhs_scale=h_scales[:, i],
                        start=True,
                        stop=True,
                    )

        def activate_h(i):
            for j in range(GRID1):
                nc.scalar.activation(
                    out=h_rows[:, i, j],
                    in_=banks[i][:, j * ROWS1 : (j + 1) * ROWS1],
                    func=RELU,
                    bias=bias[:, GRID1, GRID1 * i + j : GRID1 * i + j + 1],
                )

        def transpose_h(i):
            h_ps = psum_early.tile([P, GRID1, C_MID], BF16, tag="early")
            for j in range(GRID1):
                nc.tensor.transpose(h_ps[:, j, :], h_rows[:, i, j], sort_channels[:])
            banks[i] = h_ps

        def swap_h(i):
            h_t = work.tile([P, GRID1 * C_MID // 2], F32, align_bytes=64)
            for half in range(2):
                nc.vector.transpose(
                    out=h_t[:, half * C_MID : (half + 1) * C_MID],
                    in_=banks[i][:, 2 * half : 2 * half + 2].rearrange("p j c -> p (j c)").bitcast(F32),
                )
            banks[i] = h_t

        def group_h(i):
            nc.vector.tensor_copy(
                out=h_grp[:, i].bitcast(F32).rearrange("k (j w v) -> k j w v", j=GRID1, v=2),
                in_=banks[i][:].rearrange("k (j v w) -> k j w v", j=GRID1, v=2),
            )

        def activate_o(i):
            o_act = work.tile([P, GRID1 * ROWS2], F32, align_bytes=64)
            for j in range(GRID1):
                wanted = slice(j * P + j * ROWS2, j * P + (j + 1) * ROWS2)
                nc.scalar.activation(
                    out=o_act[:, j * ROWS2 : (j + 1) * ROWS2],
                    in_=banks[GRID1 + i][:, wanted],
                    func=RELU,
                    bias=bias[:, i, j : j + 1],
                )
            banks[GRID1 + i] = o_act

        def turn_and_store(i):
            nc.vector.transpose(out=o_out[:, i], in_=banks[GRID1 + i][:])
            for a in range(2):
                nc.sync.dma_start(
                    out=out[2 * i + a].rearrange("(j e) n y x o -> (e n y x) j o", e=2),
                    in_=o_out[a * 2 * ROWS2 : (a + 1) * 2 * ROWS2, i].rearrange("k (j o) -> k j o", j=GRID1),
                )

        def quantise_h(c):
            nc.vector.quantize_mx(out=h_codes[:, c].bitcast(FP8X4), scales=h_scales[:, c], in_=h_grp[:, c])

        def is_child(c):
            return 0 <= c < GRID1

        def is_gchild(c):
            return GRID1 <= c < 2 * GRID1

        x_banks = transpose_x()
        b_ps = transpose_biases()
        last = 2 * GRID1 - 1
        for n in range(last + 4):
            if n == 0:
                regroup(nc.scalar.copy, 0, (0, 1), ROW)
                group_x(nc.vector.tensor_copy, 0, x_banks[0])
                group_x(nc.scalar.copy, 1, x_banks[1])
                regroup(nc.scalar.copy, 0, (2,), ROW)
            elif n < last:
                regroup_on_scalar(n)
            elif n == last:
                regroup_on_scalar(n, HALVES[0])
                activate_o(n - 2 - GRID1)
                regroup_on_scalar(n, HALVES[1])
            if is_child(n - 2):
                activate_h(n - 2)
            if n == 1:
                nc.vector.quantize_mx(out=x_codes[:].bitcast(FP8X4), scales=x_scales[:], in_=x_grp[:])
            if 0 <= n - 1 < last:
                quantise_weights(n - 1)
                multiply(n - 1)
            elif n - 1 == last:
                quantise_weights(last, HALVES[0])
                multiply(last, HALVES[0])
                regroup_on_vector(last, VECTOR_UNITS[last], HALVES[1])
                quantise_weights(last, HALVES[1])
                multiply(last, HALVES[1])
            if is_child(n - 2):
                transpose_h(n - 2)
            if is_child(n):
                regroup_on_vector(n, VECTOR_UNITS[n])
                if n == 1:
                    nc.vector.tensor_copy(out=bias[:], in_=b_ps[:, :, 0:16])
            elif n < last:
                regroup_on_vector(n, VECTOR_UNITS[n][:1])
            elif n == last:
                regroup_on_vector(n, VECTOR_UNITS[n], HALVES[0])
            if is_child(n - 3):
                swap_h(n - 3)
            if is_child(n - 4):
                quantise_h(n - 4)
            if GRID1 <= n < last:
                regroup_on_vector(n, VECTOR_UNITS[n][1:])
            if is_child(n - 3):
                group_h(n - 3)
            if is_gchild(n - 3):
                turn_and_store(n - 3 - GRID1)
            if is_gchild(n - 2) and n != last:
                activate_o(n - 2 - GRID1)
